import numpy as np
import ml_dtypes


def mxq(x, axis, fmt="e4m3"):
    dtype, down = {"e4m3": (ml_dtypes.float8_e4m3fn, 7), "e5m2": (ml_dtypes.float8_e5m2, 14)}[fmt]
    v = np.moveaxis(np.asarray(x, np.float32).astype(ml_dtypes.bfloat16).astype(np.float64), axis, -1)
    blocks = v.reshape(v.shape[:-1] + (-1, 32))
    amax = np.abs(blocks).max(-1, keepdims=True)
    byte = np.maximum(np.where(amax > 0, np.frexp(amax)[1] - 1 + 127, 0) - down, 1)
    scale = np.exp2(byte - 127.0)
    codes = (blocks / scale).astype(np.float32).astype(dtype).astype(np.float64)
    return np.moveaxis((codes * scale).reshape(v.shape), -1, axis)


WIDE = False


def mx_kscale(k):
    if not WIDE:
        return np.ones(k)
    levels = np.array([10, -10, 5, -5, 0])
    if k % 512:
        return np.exp2(np.random.permutation(np.resize(levels, k // 32))).repeat(32)
    a = np.empty((k // 512, 16))
    for p in range(k // 512):
        a[p, :8] = np.random.permutation(np.resize(levels, 8))
        for g in range(8):
            far = levels[np.abs(levels - a[p, g]) >= 10]
            a[p, g + 8] = far[np.random.randint(len(far))]
    return np.exp2(a.ravel()).repeat(32)


BF16 = ml_dtypes.bfloat16


def bf(x):
    return np.asarray(x, np.float32).astype(BF16)


def f64(x):
    return np.asarray(x).astype(np.float64)


B, S, DIM, H, D = 2, 256, 2048, 16, 128
E = H * D
ROPE_THETA = 10000.0


def rope(t):
    inv_freq = 1.0 / ROPE_THETA ** (np.arange(0, D, 2) / D)
    ang = np.arange(S)[:, None] * inv_freq[None, :]
    cos = np.concatenate([np.cos(ang), np.cos(ang)], axis=-1)[None, :, None, :]
    sin = np.concatenate([np.sin(ang), np.sin(ang)], axis=-1)[None, :, None, :]
    t1, t2 = np.split(t, 2, axis=-1)
    rot = np.concatenate([-t2, t1], axis=-1)
    return t * cos + rot * sin


def draw0():
    s = mx_kscale(DIM)
    return {"x": bf(np.random.standard_normal((B, S, DIM)) * s),
            "wq": bf(np.random.standard_normal((E, DIM)) / np.sqrt(DIM) / s[None, :]),
            "wk": bf(np.random.standard_normal((E, DIM)) / np.sqrt(DIM) / s[None, :])}


def core(x, wq, wk):
    xq = mxq(f64(x), 2, "e4m3")
    q = (xq @ mxq(f64(wq), 1, "e4m3").T).reshape(B, S, H, D)
    k = (xq @ mxq(f64(wk), 1, "e4m3").T).reshape(B, S, H, D)
    return rope(q), rope(k)


def e4m3fn_bytes(y):
    return np.clip(np.asarray(y, np.float64), -448.0, 448.0).astype(np.float32).astype(ml_dtypes.float8_e4m3fn).view(np.uint8)


def e4m3fn_values(b):
    return np.asarray(b, np.uint8).view(ml_dtypes.float8_e4m3fn).astype(np.float64)


def setup_inputs():
    d = draw0()
    x0 = np.asarray(d['wq']).astype(np.float64)
    s = (np.max(np.abs(x0), axis=(0,), keepdims=True) / 448.0).astype(np.float32)
    out = {}
    for k, v in d.items():
        if k == 'wq':
            out['wq_bytes'] = e4m3fn_bytes(x0 / s.astype(np.float64))
            out['wq_scale'] = s
        else:
            out[k] = v
    return out


def reference(x, wq_bytes, wq_scale, wk):
    return core(x, e4m3fn_values(wq_bytes) * wq_scale.astype(np.float64), wk)

@@ -1,0 +1,303 @@
+from contextlib import ExitStack
+import math
+
+import concourse.mybir as mybir
+from concourse.masks import make_identity
+
+FLOPS = 2 * 512 * 2048 * 4096
+
+F32 = mybir.dt.float32
+BF16 = mybir.dt.bfloat16
+U32 = mybir.dt.uint32
+U8 = mybir.dt.uint8
+I32 = mybir.dt.int32
+FP8 = mybir.dt.float8_e4m3fn
+FP8X4 = mybir.dt.float8_e4m3fn_x4
+ALU = mybir.AluOpType
+ACTF = mybir.ActivationFunctionType
+
+P = 128
+K = 2048
+THETA = 10000.0
+NSTEP = 16
+LAG = 3
+OFF = {3: (1,), 5: (0, 1), 7: (1,), 9: (0, 1), 11: (1,), 13: (0, 1), 15: (1,)}
+X_ON_VECTOR = ((0, 0), (0, 1), (1, 0), (1, 1))
+CAST_AHEAD = 2
+
+
+def tile_multiheadattention_pa_kernel(tc, x, wq_bytes, wq_scale, wk, out_0, out_1):
+    nc = tc.nc
+    xf = x.flatten_outer_dims()
+    outs = (out_0.rearrange("b s h d -> (b s) (h d)"), out_1.rearrange("b s h d -> (b s) (h d)"))
+
+    with ExitStack() as ctx:
+        const = ctx.enter_context(tc.tile_pool(name="const", bufs=1))
+        w16p = ctx.enter_context(tc.tile_pool(name="w16p", bufs=2))
+        grp = ctx.enter_context(tc.tile_pool(name="grp", bufs=2))
+        grxp = ctx.enter_context(tc.tile_pool(name="grxp", bufs=2))
+        plp = ctx.enter_context(tc.tile_pool(name="plp", bufs=3))
+        wcp = ctx.enter_context(tc.tile_pool(name="wcp", bufs=2))
+        rp = ctx.enter_context(tc.tile_pool(name="rp", bufs=4))
+        pst = ctx.enter_context(tc.psum_pool(name="pst", bufs=4))
+        psa = ctx.enter_context(tc.psum_pool(name="psa", bufs=4))
+        ctx.enter_context(tc.manual_schedule())
+
+        sc = const.tile([P, 4, 4], F32, name="sc")
+        nc.scalar.dma_start(out=sc[:], in_=wq_scale.rearrange("o (g p t) -> p (o g) t", p=P, t=4))
+        wqb = []
+        wkb = []
+        xr = []
+        for b in range(8):
+            wqb.append(const.tile([P, 2, K], U8, name="wqb%d" % b))
+            wkb.append(const.tile([P, 2, K], BF16, name="wkb%d" % b))
+        for m in range(4):
+            xr.append(const.tile([P, K], BF16, name="xr%d" % m))
+
+        def load_w(b):
+            rows = slice(256 * b, 256 * (b + 1))
+            nc.sync.dma_start(out=wqb[b][:], in_=wq_bytes[rows, :].rearrange("(r p) k -> p r k", p=P))
+            nc.sync.dma_start(out=wkb[b][:], in_=wk[rows, :].rearrange("(r p) k -> p r k", p=P))
+
+        for g in range(4):
+            nc.sync.dma_start(out=xr[0][:, 512 * g : 512 * (g + 1)], in_=xf[0:P, 512 * g : 512 * (g + 1)])
+        nc.sync.dma_start(out=wqb[0][:], in_=wq_bytes[0:256, :].rearrange("(r p) k -> p r k", p=P))
+        nc.sync.dma_start(out=xr[1][:], in_=xf[P : 2 * P, :])
+        nc.sync.dma_start(out=wkb[0][:], in_=wk[0:256, :].rearrange("(r p) k -> p r k", p=P))
+        nc.sync.dma_start(out=xr[2][:], in_=xf[2 * P : 3 * P, :])
+        nc.sync.dma_start(out=xr[3][:], in_=xf[3 * P : 4 * P, :])
+        for b in range(1, 8):
+            load_w(b)
+
+        zero = const.tile([P, 1], F32, name="zero")
+        nc.vector.memset(zero[:], 0.0)
+        warm = const.tile([P, 1], F32, name="warm")
+        nc.scalar.activation(out=warm[:], in_=zero[:], func=ACTF.Sin)
+
+        ident = const.tile([P, P], F32, name="ident")
+        make_identity(nc, ident[:])
+
+        pos_f = const.tile([P, 2], F32, name="pos_f")
+        nc.gpsimd.iota(pos_f[:], pattern=[[P, 2]], base=0, channel_multiplier=1, allow_small_or_imprecise_dtypes=True)
+        freq = const.tile([P, 64], F32, name="freq")
+        nc.gpsimd.memset(freq[:, 0:1], 1.0)
+        w = 1
+        while w < 64:
+            nc.gpsimd.tensor_scalar(
+                out=freq[:, w : 2 * w], in0=freq[:, 0:w], scalar1=THETA ** (-w / 64.0), scalar2=0.0,
+                op0=ALU.mult, op1=ALU.add,
+            )
+            w *= 2
+        ang = const.tile([P, 2, 2, 64], F32, name="ang")
+        for a in range(2):
+            for f in range(2):
+                nc.gpsimd.tensor_scalar(
+                    out=ang[:, a, f, :], in0=freq[:], scalar1=pos_f[:, a : a + 1], scalar2=f * math.pi / 2.0,
+                    op0=ALU.mult, op1=ALU.add,
+                )
+        angf = ang[:].rearrange("p a f j -> p (a f j)")
+        turns = const.tile([P, 256], F32, name="turns")
+        nc.gpsimd.tensor_scalar(out=turns[:], in0=angf, scalar1=1.0 / math.pi, scalar2=0.25, op0=ALU.mult, op1=ALU.add)
+        n_i = const.tile([P, 256], I32, name="n_i")
+        red = const.tile([P, 256], F32, name="red")
+        red2 = const.tile([P, 256], F32, name="red2")
+        par = const.tile([P, 256], I32, name="par")
+        sgn = const.tile([P, 2, 2, 64], F32, name="sgn")
+        sn = const.tile([P, 2, 2, 64], F32, name="sn")
+        tab = const.tile([P, 2, 2, 2, 64], F32, name="tab")
+        pi_hi = math.floor(math.pi * 16384.0) / 16384.0
+        pi_lo = math.pi - pi_hi
+
+        def table_step(i):
+            if i == 0:
+                nc.vector.tensor_copy(out=n_i[:], in_=turns[:])
+            elif i == 1:
+                nc.vector.tensor_single_scalar(out=par[:], in_=n_i[:], scalar=1, op=ALU.bitwise_and)
+            elif i == 2:
+                nc.vector.scalar_tensor_tensor(
+                    out=red[:], in0=n_i[:], scalar=-pi_hi, in1=angf, op0=ALU.mult, op1=ALU.add
+                )
+            elif i == 3:
+                nc.vector.tensor_scalar(
+                    out=sgn[:].rearrange("p a f j -> p (a f j)"), in0=par[:], scalar1=-2.0, scalar2=1.0,
+                    op0=ALU.mult, op1=ALU.add,
+                )
+            else:
+                nc.vector.scalar_tensor_tensor(
+                    out=red2[:], in0=n_i[:], scalar=-pi_lo, in1=red[:], op0=ALU.mult, op1=ALU.add
+                )
+
+        def tables_finish():
+            nc.scalar.activation(out=sn[:].rearrange("p a f j -> p (a f j)"), in_=red2[:], func=ACTF.Sin)
+            for wv in range(2):
+                nc.gpsimd.tensor_tensor(out=tab[:, :, 0, wv, :], in0=sn[:, :, 1, :], in1=sgn[:, :, 1, :], op=ALU.mult)
+            nc.gpsimd.tensor_tensor(out=tab[:, :, 1, 0, :], in0=sn[:, :, 0, :], in1=sgn[:, :, 0, :], op=ALU.mult)
+            nc.gpsimd.tensor_scalar(
+                out=tab[:, :, 1, 1, :], in0=tab[:, :, 1, 0, :], scalar1=-1.0, scalar2=0.0, op0=ALU.mult, op1=ALU.add
+            )
+
+        xc = []
+        xs = []
+        for m in range(4):
+            xc.append(const.tile([P, 512], U32, name="xc%d" % m, align_bytes=64))
+            xs.append(const.tile([P, 512], U8, name="xs%d" % m, align_bytes=64))
+
+        def transposes(bank, words2, g):
+            for c in range(2):
+                for u in range(2):
+                    nc.tensor.transpose(bank[:, u, c, :], words2[c][:, 256 * g + u : 256 * (g + 1) : 2], ident[:])
+
+        grxs = {}
+
+        def x_turn(m):
+            grx = grxp.tile([P, 4, P, 4], BF16, name="grx", tag="grx", align_bytes=64)
+            grxs[m] = grx
+            grx_w = grx[:].bitcast(F32)
+            words = xr[m][:].bitcast(F32)
+            for gp in range(2):
+                bank = pst.tile([P, 2, 2, P], F32, name="tb", tag="tb")
+                for g2 in range(2):
+                    g = 2 * gp + g2
+                    for u in range(2):
+                        nc.tensor.transpose(bank[:, u, g2, :], words[:, 256 * g + u : 256 * (g + 1) : 2], ident[:])
+                if (m, gp) in X_ON_VECTOR:
+                    nc.vector.tensor_copy(
+                        out=grx_w[:, 2 * gp : 2 * gp + 2, :, :], in_=bank[:].rearrange("p u g r -> p g r u")
+                    )
+                else:
+                    nc.scalar.copy(
+                        out=grx_w[:, 2 * gp : 2 * gp + 2, :, :], in_=bank[:].rearrange("p u g r -> p g r u")
+                    )
+
+        def x_quant(m):
+            nc.vector.quantize_mx(
+                out=xc[m][:].bitcast(FP8X4), scales=xs[m][:], in_=grxs[m][:].rearrange("p g r t -> p (g r t)")
+            )
+
+        w16 = {}
+        gr = {}
+        wc = {}
+        ws = {}
+
+        def cast(s):
+            b, gp = divmod(s, 2)
+            if gp == 0:
+                w16[b] = w16p.tile([P, 2, K], BF16, name="w16", tag="w16")
+            cols = slice(1024 * gp, 1024 * (gp + 1))
+            for r2 in range(2):
+                nc.scalar.copy(out=w16[b][:, r2, cols], in_=wqb[b][:, r2, cols].bitcast(FP8))
+
+        def turn(s, fill=()):
+            b, gp = divmod(s, 2)
+            if gp == 0:
+                gr[b] = grp.tile([P, 4, 512, 4], BF16, name="gr", tag="gr", align_bytes=64)
+            g_t = gr[b]
+            g_w = g_t[:].bitcast(F32)
+            qw = [w16[b][:, c, :].bitcast(F32) for c in range(2)]
+            kw = [wkb[b][:, c, :].bitcast(F32) for c in range(2)]
+            banks = []
+            for words2 in (qw, kw):
+                for g2 in range(2):
+                    bank = pst.tile([P, 2, 2, P], F32, name="tb", tag="tb")
+                    transposes(bank, words2, 2 * gp + g2)
+                    banks.append(bank)
+            planes = {}
+            for g2 in range(2):
+                g = 2 * gp + g2
+                if g2 in OFF.get(s, ()):
+                    planes[g] = plp.tile([P, 4, 256], BF16, name="pl", tag="pl")
+                    bv = banks[g2][:].bitcast(BF16).rearrange("p u c (r e) -> p u e (c r)", e=2)
+                    for t in range(4):
+                        nc.scalar.activation(
+                            out=planes[g][:, t, :], in_=bv[:, t // 2, t % 2, :], func=ACTF.Copy, scale=sc[:, g, t : t + 1]
+                        )
+                else:
+                    nc.vector.tensor_tensor(
+                        out=g_t[:, g, 0:256, :].rearrange("p r (u e) -> p r u e", e=2),
+                        in0=banks[g2][:].bitcast(BF16).rearrange("p u c (r e) -> p (c r) u e", e=2),
+                        in1=sc[:, g, :].rearrange("p (u e) -> p u e", e=2).unsqueeze(1).to_broadcast([P, 256, 2, 2]),
+                        op=ALU.mult,
+                    )
+                    for i in fill[g2 : g2 + 1]:
+                        table_step(i)
+            for g2 in range(2):
+                g = 2 * gp + g2
+                nc.scalar.copy(out=g_w[:, g, 256:512, :], in_=banks[2 + g2][:].rearrange("p u c r -> p (c r) u"))
+            for g in sorted(planes):
+                nc.scalar.copy(out=g_t[:, g, 0:256, :], in_=planes[g][:].rearrange("p t r -> p r t"))
+
+        def quant(s):
+            b, gp = divmod(s, 2)
+            if gp == 0:
+                wc[b] = wcp.tile([P, 4, 512], U32, name="wc", tag="wc", align_bytes=64)
+                ws[b] = wcp.tile([P, 4, 512], U8, name="ws", tag="ws", align_bytes=64)
+            gs = slice(2 * gp, 2 * gp + 2)
+            nc.vector.quantize_mx(
+                out=wc[b][:, gs, :].rearrange("p g n -> p (g n)").bitcast(FP8X4),
+                scales=ws[b][:, gs, :].rearrange("p g n -> p (g n)"),
+                in_=gr[b][:, gs, :, :].rearrange("p g n t -> p (g n t)"),
+            )
+
+        def project(b, m):
+            acc = psa.tile([P, 512], F32, name="acc", tag="acc")
+            for g in range(4):
+                cols = slice(P * g, P * (g + 1))
+                nc.tensor.matmul_mx(
+                    out=acc[:],
+                    lhsT=xc[m][:, cols].bitcast(FP8X4),
+                    lhsT_scale=xs[m][:, cols],
+                    rhs=wc[b][:, g, :].bitcast(FP8X4),
+                    rhs_scale=ws[b][:, g, :],
+                    start=(g == 0),
+                    stop=(g == 3),
+                )
+            return acc
+
+        def rope(b, m, acc, last):
+            a = m % 2
+            pq = rp.tile([P, 2, 4, 2, 64], F32, name="pq", tag="pq")
+            nc.vector.tensor_tensor(
+                out=pq[:].rearrange("p q h w j -> p q h (w j)"),
+                in0=acc[:].rearrange("p (h d) -> p h d", d=P).unsqueeze(1).to_broadcast([P, 2, 4, P]),
+                in1=tab[:, a].rearrange("p q w j -> p q (w j)").unsqueeze(2).to_broadcast([P, 2, 4, P]),
+                op=ALU.mult,
+            )
+            adder = nc.vector if last else nc.gpsimd
+            adder.tensor_tensor(out=pq[:, 0], in0=pq[:, 0], in1=pq[:, 1, :, ::-1, :], op=ALU.add)
+            for o in range(2):
+                nc.sync.dma_start(
+                    out=outs[o][P * m : P * (m + 1), 256 * b : 256 * (b + 1)],
+                    in_=pq[:, 0, 2 * o : 2 * o + 2].rearrange("p h w j -> p (h w j)"),
+                )
+
+        for s in range(NSTEP + LAG):
+            if s == 0:
+                x_turn(0)
+                x_turn(1)
+                x_quant(0)
+                x_quant(1)
+                for s0 in range(CAST_AHEAD):
+                    cast(s0)
+            if s == 1:
+                x_turn(2)
+                x_turn(3)
+                x_quant(2)
+                table_step(0)
+                x_quant(3)
+                table_step(1)
+                table_step(2)
+            if s < NSTEP:
+                turn(s, (3, 4) if s == 1 else ())
+            if s == 1:
+                tables_finish()
+            if s + CAST_AHEAD < NSTEP:
+                cast(s + CAST_AHEAD)
+            if s % 2 == 0 and 2 <= s <= NSTEP:
+                quant(s - 2)
+                quant(s - 1)
+            j = s - LAG
+            if j >= 0:
+                b, half = divmod(j, 2)
+                for m in (2 * half, 2 * half + 1):
+                    acc = project(b, m)
+                    rope(b, m, acc, j == NSTEP - 1 and m == 3)

@@ -33,12 +33,12 @@ def tile_multiheadattention_pa_kernel(tc, x, wq_bytes, wq_scale, wk, out_0, out_
 
     with ExitStack() as ctx:
         const = ctx.enter_context(tc.tile_pool(name="const", bufs=1))
-        w16p = ctx.enter_context(tc.tile_pool(name="w16p", bufs=2))
+        w16p = ctx.enter_context(tc.tile_pool(name="w16p", bufs=3))
         grp = ctx.enter_context(tc.tile_pool(name="grp", bufs=2))
         grxp = ctx.enter_context(tc.tile_pool(name="grxp", bufs=2))
         plp = ctx.enter_context(tc.tile_pool(name="plp", bufs=3))
         wcp = ctx.enter_context(tc.tile_pool(name="wcp", bufs=2))
-        rp = ctx.enter_context(tc.tile_pool(name="rp", bufs=4))
+        rp = ctx.enter_context(tc.tile_pool(name="rp", bufs=6))
         pst = ctx.enter_context(tc.psum_pool(name="pst", bufs=4))
         psa = ctx.enter_context(tc.psum_pool(name="psa", bufs=4))
         ctx.enter_context(tc.manual_schedule())
@@ -48,26 +48,39 @@ def tile_multiheadattention_pa_kernel(tc, x, wq_bytes, wq_scale, wk, out_0, out_
         wqb = []
         wkb = []
         xr = []
-        for b in range(8):
-            wqb.append(const.tile([P, 2, K], U8, name="wqb%d" % b))
-            wkb.append(const.tile([P, 2, K], BF16, name="wkb%d" % b))
+        for s in range(NSTEP):
+            wqb.append(const.tile([P, 2, 1024], U8, name="wqb%d" % s))
+            wkb.append(const.tile([P, 2, 1024], BF16, name="wkb%d" % s))
         for m in range(4):
-            xr.append(const.tile([P, K], BF16, name="xr%d" % m))
+            xr.append(rp.tile([P, K], BF16, name="xr%d" % m, tag="pq"))
 
-        def load_w(b):
-            rows = slice(256 * b, 256 * (b + 1))
-            nc.sync.dma_start(out=wqb[b][:], in_=wq_bytes[rows, :].rearrange("(r p) k -> p r k", p=P))
-            nc.sync.dma_start(out=wkb[b][:], in_=wk[rows, :].rearrange("(r p) k -> p r k", p=P))
+        def load_q(s):
+            b, gp = divmod(s, 2)
+            nc.sync.dma_start(
+                out=wqb[s][:],
+                in_=wq_bytes[256 * b : 256 * (b + 1), 1024 * gp : 1024 * (gp + 1)].rearrange("(r p) k -> p r k", p=P),
+            )
 
-        for g in range(4):
-            nc.sync.dma_start(out=xr[0][:, 512 * g : 512 * (g + 1)], in_=xf[0:P, 512 * g : 512 * (g + 1)])
-        nc.sync.dma_start(out=wqb[0][:], in_=wq_bytes[0:256, :].rearrange("(r p) k -> p r k", p=P))
-        nc.sync.dma_start(out=xr[1][:], in_=xf[P : 2 * P, :])
-        nc.sync.dma_start(out=wkb[0][:], in_=wk[0:256, :].rearrange("(r p) k -> p r k", p=P))
-        nc.sync.dma_start(out=xr[2][:], in_=xf[2 * P : 3 * P, :])
-        nc.sync.dma_start(out=xr[3][:], in_=xf[3 * P : 4 * P, :])
-        for b in range(1, 8):
-            load_w(b)
+        def load_k(s):
+            b, gp = divmod(s, 2)
+            nc.sync.dma_start(
+                out=wkb[s][:],
+                in_=wk[256 * b : 256 * (b + 1), 1024 * gp : 1024 * (gp + 1)].rearrange("(r p) k -> p r k", p=P),
+            )
+
+        def load_x(m, pieces):
+            w = K // pieces
+            for i in range(pieces):
+                nc.sync.dma_start(out=xr[m][:, w * i : w * (i + 1)], in_=xf[P * m : P * (m + 1), w * i : w * (i + 1)])
+
+        load_q(0)
+        load_x(0, 2)
+        load_k(0)
+        for s in range(1, NSTEP):
+            load_q(s)
+            load_k(s)
+            if s < 4:
+                load_x(s, 1)
 
         zero = const.tile([P, 1], F32, name="zero")
         nc.vector.memset(zero[:], 0.0)
@@ -180,12 +193,10 @@ def tile_multiheadattention_pa_kernel(tc, x, wq_bytes, wq_scale, wk, out_0, out_
         ws = {}
 
         def cast(s):
-            b, gp = divmod(s, 2)
-            if gp == 0:
-                w16[b] = w16p.tile([P, 2, K], BF16, name="w16", tag="w16")
-            cols = slice(1024 * gp, 1024 * (gp + 1))
-            for r2 in range(2):
-                nc.scalar.copy(out=w16[b][:, r2, cols], in_=wqb[b][:, r2, cols].bitcast(FP8))
+            w16[s] = w16p.tile([P, 2, 1024], BF16, name="w16", tag="w16")
+            nc.scalar.copy(
+                out=w16[s][:].rearrange("p r k -> p (r k)"), in_=wqb[s][:].rearrange("p r k -> p (r k)").bitcast(FP8)
+            )
 
         def turn(s, fill=()):
             b, gp = divmod(s, 2)
@@ -193,13 +204,13 @@ def tile_multiheadattention_pa_kernel(tc, x, wq_bytes, wq_scale, wk, out_0, out_
                 gr[b] = grp.tile([P, 4, 512, 4], BF16, name="gr", tag="gr", align_bytes=64)
             g_t = gr[b]
             g_w = g_t[:].bitcast(F32)
-            qw = [w16[b][:, c, :].bitcast(F32) for c in range(2)]
-            kw = [wkb[b][:, c, :].bitcast(F32) for c in range(2)]
+            qw = [w16[s][:, c, :].bitcast(F32) for c in range(2)]
+            kw = [wkb[s][:, c, :].bitcast(F32) for c in range(2)]
             banks = []
             for words2 in (qw, kw):
                 for g2 in range(2):
                     bank = pst.tile([P, 2, 2, P], F32, name="tb", tag="tb")
-                    transposes(bank, words2, 2 * gp + g2)
+                    transposes(bank, words2, g2)
                     banks.append(bank)
             planes = {}
             for g2 in range(2):
@@ -272,26 +283,22 @@ def tile_multiheadattention_pa_kernel(tc, x, wq_bytes, wq_scale, wk, out_0, out_
 
         for s in range(NSTEP + LAG):
             if s == 0:
-                x_turn(0)
-                x_turn(1)
-                x_quant(0)
-                x_quant(1)
                 for s0 in range(CAST_AHEAD):
                     cast(s0)
+            if s < 4:
+                x_turn(s)
             if s == 1:
-                x_turn(2)
-                x_turn(3)
-                x_quant(2)
                 table_step(0)
-                x_quant(3)
-                table_step(1)
-                table_step(2)
             if s < NSTEP:
-                turn(s, (3, 4) if s == 1 else ())
+                turn(s, (1, 2) if s == 1 else (4,) if s == 2 else ())
+            if s < 4:
+                x_quant(s)
             if s == 1:
-                tables_finish()
+                table_step(3)
             if s + CAST_AHEAD < NSTEP:
                 cast(s + CAST_AHEAD)
+            if s == 2:
+                tables_finish()
             if s % 2 == 0 and 2 <= s <= NSTEP:
                 quant(s - 2)
                 quant(s - 1)

@@ -235,7 +235,10 @@ def tile_multiheadattention_pa_kernel(tc, x, wq_bytes, wq_scale, wk, out_0, out_
                 g = 2 * gp + g2
                 nc.scalar.copy(out=g_w[:, g, 256:512, :], in_=banks[2 + g2][:].rearrange("p u c r -> p (c r) u"))
             for g in sorted(planes):
-                nc.scalar.copy(out=g_t[:, g, 0:256, :], in_=planes[g][:].rearrange("p t r -> p r t"))
+                nc.scalar.copy(
+                    out=g_t[:, g, 0:256, :].rearrange("p (c i) t -> p c t i", i=4),
+                    in_=planes[g][:].rearrange("p t (c i) -> p c t i", i=4),
+                )
 
         def quant(s):
             b, gp = divmod(s, 2)

@@ -198,7 +198,7 @@ def tile_multiheadattention_pa_kernel(tc, x, wq_bytes, wq_scale, wk, out_0, out_
                 out=w16[s][:].rearrange("p r k -> p (r k)"), in_=wqb[s][:].rearrange("p r k -> p (r k)").bitcast(FP8)
             )
 
-        def turn(s, fill=()):
+        def turn(s, fill, mm):
             b, gp = divmod(s, 2)
             if gp == 0:
                 gr[b] = grp.tile([P, 4, 512, 4], BF16, name="gr", tag="gr", align_bytes=64)
@@ -207,11 +207,14 @@ def tile_multiheadattention_pa_kernel(tc, x, wq_bytes, wq_scale, wk, out_0, out_
             qw = [w16[s][:, c, :].bitcast(F32) for c in range(2)]
             kw = [wkb[s][:, c, :].bitcast(F32) for c in range(2)]
             banks = []
-            for words2 in (qw, kw):
+            accs = []
+            for wi, words2 in enumerate((qw, kw)):
                 for g2 in range(2):
                     bank = pst.tile([P, 2, 2, P], F32, name="tb", tag="tb")
                     transposes(bank, words2, g2)
                     banks.append(bank)
+                for bm in mm[wi : wi + 1]:
+                    accs.append(project(bm[0], bm[1]))
             planes = {}
             for g2 in range(2):
                 g = 2 * gp + g2
@@ -239,6 +242,7 @@ def tile_multiheadattention_pa_kernel(tc, x, wq_bytes, wq_scale, wk, out_0, out_
                     out=g_t[:, g, 0:256, :].rearrange("p (c i) t -> p c t i", i=4),
                     in_=planes[g][:].rearrange("p t (c i) -> p c t i", i=4),
                 )
+            return accs
 
         def quant(s):
             b, gp = divmod(s, 2)
@@ -292,8 +296,12 @@ def tile_multiheadattention_pa_kernel(tc, x, wq_bytes, wq_scale, wk, out_0, out_
                 x_turn(s)
             if s == 1:
                 table_step(0)
+            j = s - LAG
+            mm = [(j // 2, 2 * (j % 2)), (j // 2, 2 * (j % 2) + 1)] if j >= 0 else []
             if s < NSTEP:
-                turn(s, (1, 2) if s == 1 else (4,) if s == 2 else ())
+                accs = turn(s, (1, 2) if s == 1 else (4,) if s == 2 else (), mm)
+            else:
+                accs = [project(bm[0], bm[1]) for bm in mm]
             if s < 4:
                 x_quant(s)
             if s == 1:
@@ -305,9 +313,5 @@ def tile_multiheadattention_pa_kernel(tc, x, wq_bytes, wq_scale, wk, out_0, out_
             if s % 2 == 0 and 2 <= s <= NSTEP:
                 quant(s - 2)
                 quant(s - 1)
-            j = s - LAG
-            if j >= 0:
-                b, half = divmod(j, 2)
-                for m in (2 * half, 2 * half + 1):
-                    acc = project(b, m)
-                    rope(b, m, acc, j == NSTEP - 1 and m == 3)
+            for bm, acc in zip(mm, accs):
+                rope(bm[0], bm[1], acc, j == NSTEP - 1 and bm[1] == 3)

@@ -21,7 +21,7 @@ K = 2048
 THETA = 10000.0
 NSTEP = 16
 LAG = 3
-OFF = {3: (1,), 5: (0, 1), 7: (1,), 9: (0, 1), 11: (1,), 13: (0, 1), 15: (1,)}
+OFF = {3: (1,), 5: (0, 1), 7: (0, 1), 9: (0, 1), 11: (0, 1), 13: (0, 1), 15: (0, 1)}
 X_ON_VECTOR = ((0, 0), (0, 1), (1, 0), (1, 1))
 CAST_AHEAD = 2
 

@@ -292,6 +292,8 @@ def tile_multiheadattention_pa_kernel(tc, x, wq_bytes, wq_scale, wk, out_0, out_
             if s == 0:
                 for s0 in range(CAST_AHEAD):
                     cast(s0)
+            if s == 2:
+                tables_finish()
             if s < 4:
                 x_turn(s)
             if s == 1:
@@ -299,17 +301,16 @@ def tile_multiheadattention_pa_kernel(tc, x, wq_bytes, wq_scale, wk, out_0, out_
             j = s - LAG
             mm = [(j // 2, 2 * (j % 2)), (j // 2, 2 * (j % 2) + 1)] if j >= 0 else []
             if s < NSTEP:
-                accs = turn(s, (1, 2) if s == 1 else (4,) if s == 2 else (), mm)
+                accs = turn(s, (1, 2) if s == 1 else (), mm)
             else:
                 accs = [project(bm[0], bm[1]) for bm in mm]
             if s < 4:
                 x_quant(s)
             if s == 1:
                 table_step(3)
+                table_step(4)
             if s + CAST_AHEAD < NSTEP:
                 cast(s + CAST_AHEAD)
-            if s == 2:
-                tables_finish()
             if s % 2 == 0 and 2 <= s <= NSTEP:
                 quant(s - 2)
                 quant(s - 1)

@@ -20,10 +20,12 @@ P = 128
 K = 2048
 THETA = 10000.0
 NSTEP = 16
-LAG = 3
-OFF = {3: (1,), 5: (0, 1), 7: (0, 1), 9: (0, 1), 11: (0, 1), 13: (0, 1), 15: (0, 1)}
-X_ON_VECTOR = ((0, 0), (0, 1), (1, 0), (1, 1))
+LAG = 2
+SCALAR_BANKS = {s: (1,) for s in range(2, 16)}
+X_ON_VECTOR = (0, 1)
 CAST_AHEAD = 2
+ROPE_BUFS = 12
+G_IL = ()
 
 
 def tile_multiheadattention_pa_kernel(tc, x, wq_bytes, wq_scale, wk, out_0, out_1):
@@ -34,13 +36,12 @@ def tile_multiheadattention_pa_kernel(tc, x, wq_bytes, wq_scale, wk, out_0, out_
     with ExitStack() as ctx:
         const = ctx.enter_context(tc.tile_pool(name="const", bufs=1))
         w16p = ctx.enter_context(tc.tile_pool(name="w16p", bufs=3))
-        grp = ctx.enter_context(tc.tile_pool(name="grp", bufs=2))
+        grp = ctx.enter_context(tc.tile_pool(name="grp", bufs=3))
         grxp = ctx.enter_context(tc.tile_pool(name="grxp", bufs=2))
         plp = ctx.enter_context(tc.tile_pool(name="plp", bufs=3))
-        wcp = ctx.enter_context(tc.tile_pool(name="wcp", bufs=2))
-        rp = ctx.enter_context(tc.tile_pool(name="rp", bufs=6))
-        pst = ctx.enter_context(tc.psum_pool(name="pst", bufs=4))
-        psa = ctx.enter_context(tc.psum_pool(name="psa", bufs=4))
+        wcp = ctx.enter_context(tc.tile_pool(name="wcp", bufs=3))
+        rp = ctx.enter_context(tc.tile_pool(name="rp", bufs=ROPE_BUFS))
+        ps = ctx.enter_context(tc.psum_pool(name="ps", bufs=8))
         ctx.enter_context(tc.manual_schedule())
 
         sc = const.tile([P, 4, 4], F32, name="sc")
@@ -49,24 +50,16 @@ def tile_multiheadattention_pa_kernel(tc, x, wq_bytes, wq_scale, wk, out_0, out_
         wkb = []
         xr = []
         for s in range(NSTEP):
-            wqb.append(const.tile([P, 2, 1024], U8, name="wqb%d" % s))
-            wkb.append(const.tile([P, 2, 1024], BF16, name="wkb%d" % s))
+            wqb.append(const.tile([P, K], U8, name="wqb%d" % s))
+            wkb.append(const.tile([P, K], BF16, name="wkb%d" % s))
         for m in range(4):
             xr.append(rp.tile([P, K], BF16, name="xr%d" % m, tag="pq"))
 
         def load_q(s):
-            b, gp = divmod(s, 2)
-            nc.sync.dma_start(
-                out=wqb[s][:],
-                in_=wq_bytes[256 * b : 256 * (b + 1), 1024 * gp : 1024 * (gp + 1)].rearrange("(r p) k -> p r k", p=P),
-            )
+            nc.sync.dma_start(out=wqb[s][:], in_=wq_bytes[P * s : P * (s + 1), :])
 
         def load_k(s):
-            b, gp = divmod(s, 2)
-            nc.sync.dma_start(
-                out=wkb[s][:],
-                in_=wk[256 * b : 256 * (b + 1), 1024 * gp : 1024 * (gp + 1)].rearrange("(r p) k -> p r k", p=P),
-            )
+            nc.sync.dma_start(out=wkb[s][:], in_=wk[P * s : P * (s + 1), :])
 
         def load_x(m, pieces):
             w = K // pieces
@@ -76,11 +69,14 @@ def tile_multiheadattention_pa_kernel(tc, x, wq_bytes, wq_scale, wk, out_0, out_
         load_q(0)
         load_x(0, 2)
         load_k(0)
-        for s in range(1, NSTEP):
+        load_x(1, 1)
+        load_q(1)
+        load_x(2, 1)
+        load_k(1)
+        load_x(3, 1)
+        for s in range(2, NSTEP):
             load_q(s)
             load_k(s)
-            if s < 4:
-                load_x(s, 1)
 
         zero = const.tile([P, 1], F32, name="zero")
         nc.vector.memset(zero[:], 0.0)
@@ -105,10 +101,10 @@ def tile_multiheadattention_pa_kernel(tc, x, wq_bytes, wq_scale, wk, out_0, out_
         for a in range(2):
             for f in range(2):
                 nc.gpsimd.tensor_scalar(
-                    out=ang[:, a, f, :], in0=freq[:], scalar1=pos_f[:, a : a + 1], scalar2=f * math.pi / 2.0,
+                    out=ang[:, f, a, :], in0=freq[:], scalar1=pos_f[:, a : a + 1], scalar2=f * math.pi / 2.0,
                     op0=ALU.mult, op1=ALU.add,
                 )
-        angf = ang[:].rearrange("p a f j -> p (a f j)")
+        angf = ang[:].rearrange("p f a j -> p (f a j)")
         turns = const.tile([P, 256], F32, name="turns")
         nc.gpsimd.tensor_scalar(out=turns[:], in0=angf, scalar1=1.0 / math.pi, scalar2=0.25, op0=ALU.mult, op1=ALU.add)
         n_i = const.tile([P, 256], I32, name="n_i")
@@ -132,7 +128,7 @@ def tile_multiheadattention_pa_kernel(tc, x, wq_bytes, wq_scale, wk, out_0, out_
                 )
             elif i == 3:
                 nc.vector.tensor_scalar(
-                    out=sgn[:].rearrange("p a f j -> p (a f j)"), in0=par[:], scalar1=-2.0, scalar2=1.0,
+                    out=sgn[:].rearrange("p f a j -> p (f a j)"), in0=par[:], scalar1=-2.0, scalar2=1.0,
                     op0=ALU.mult, op1=ALU.add,
                 )
             else:
@@ -141,12 +137,12 @@ def tile_multiheadattention_pa_kernel(tc, x, wq_bytes, wq_scale, wk, out_0, out_
                 )
 
         def tables_finish():
-            nc.scalar.activation(out=sn[:].rearrange("p a f j -> p (a f j)"), in_=red2[:], func=ACTF.Sin)
+            nc.scalar.activation(out=sn[:].rearrange("p f a j -> p (f a j)"), in_=red2[:], func=ACTF.Sin)
             for wv in range(2):
-                nc.gpsimd.tensor_tensor(out=tab[:, :, 0, wv, :], in0=sn[:, :, 1, :], in1=sgn[:, :, 1, :], op=ALU.mult)
-            nc.gpsimd.tensor_tensor(out=tab[:, :, 1, 0, :], in0=sn[:, :, 0, :], in1=sgn[:, :, 0, :], op=ALU.mult)
+                nc.gpsimd.tensor_tensor(out=tab[:, 0, :, wv, :], in0=sn[:, 1], in1=sgn[:, 1], op=ALU.mult)
+            nc.gpsimd.tensor_tensor(out=tab[:, 1, :, 0, :], in0=sn[:, 0], in1=sgn[:, 0], op=ALU.mult)
             nc.gpsimd.tensor_scalar(
-                out=tab[:, :, 1, 1, :], in0=tab[:, :, 1, 0, :], scalar1=-1.0, scalar2=0.0, op0=ALU.mult, op1=ALU.add
+                out=tab[:, 1, :, 1, :], in0=tab[:, 1, :, 0, :], scalar1=-1.0, scalar2=0.0, op0=ALU.mult, op1=ALU.add
             )
 
         xc = []
@@ -155,32 +151,23 @@ def tile_multiheadattention_pa_kernel(tc, x, wq_bytes, wq_scale, wk, out_0, out_
             xc.append(const.tile([P, 512], U32, name="xc%d" % m, align_bytes=64))
             xs.append(const.tile([P, 512], U8, name="xs%d" % m, align_bytes=64))
 
-        def transposes(bank, words2, g):
-            for c in range(2):
+        def turn_half(words, gh):
+            bank = ps.tile([P, 2, 2, P], F32, name="tb", tag="ps")
+            for g2 in range(2):
+                g = 2 * gh + g2
                 for u in range(2):
-                    nc.tensor.transpose(bank[:, u, c, :], words2[c][:, 256 * g + u : 256 * (g + 1) : 2], ident[:])
+                    nc.tensor.transpose(bank[:, u, g2, :], words[:, 256 * g + u : 256 * (g + 1) : 2], ident[:])
+            return bank
 
         grxs = {}
 
         def x_turn(m):
-            grx = grxp.tile([P, 4, P, 4], BF16, name="grx", tag="grx", align_bytes=64)
-            grxs[m] = grx
-            grx_w = grx[:].bitcast(F32)
-            words = xr[m][:].bitcast(F32)
-            for gp in range(2):
-                bank = pst.tile([P, 2, 2, P], F32, name="tb", tag="tb")
-                for g2 in range(2):
-                    g = 2 * gp + g2
-                    for u in range(2):
-                        nc.tensor.transpose(bank[:, u, g2, :], words[:, 256 * g + u : 256 * (g + 1) : 2], ident[:])
-                if (m, gp) in X_ON_VECTOR:
-                    nc.vector.tensor_copy(
-                        out=grx_w[:, 2 * gp : 2 * gp + 2, :, :], in_=bank[:].rearrange("p u g r -> p g r u")
-                    )
-                else:
-                    nc.scalar.copy(
-                        out=grx_w[:, 2 * gp : 2 * gp + 2, :, :], in_=bank[:].rearrange("p u g r -> p g r u")
-                    )
+            grxs[m] = grxp.tile([P, 4, P, 4], BF16, name="grx", tag="grx", align_bytes=64)
+            grx_w = grxs[m][:].bitcast(F32)
+            for gh in range(2):
+                bank = turn_half(xr[m][:].bitcast(F32), gh)
+                copier = nc.vector.tensor_copy if m in X_ON_VECTOR else nc.scalar.copy
+                copier(out=grx_w[:, 2 * gh : 2 * gh + 2, :, :], in_=bank[:].rearrange("p u g r -> p g r u"))
 
         def x_quant(m):
             nc.vector.quantize_mx(
@@ -193,126 +180,136 @@ def tile_multiheadattention_pa_kernel(tc, x, wq_bytes, wq_scale, wk, out_0, out_
         ws = {}
 
         def cast(s):
-            w16[s] = w16p.tile([P, 2, 1024], BF16, name="w16", tag="w16")
-            nc.scalar.copy(
-                out=w16[s][:].rearrange("p r k -> p (r k)"), in_=wqb[s][:].rearrange("p r k -> p (r k)").bitcast(FP8)
+            w16[s] = w16p.tile([P, K], BF16, name="w16", tag="w16")
+            nc.scalar.copy(out=w16[s][:], in_=wqb[s][:].bitcast(FP8))
+
+        def scale_on_vector(s, gh, bank):
+            gs = slice(2 * gh, 2 * gh + 2)
+            nc.vector.tensor_tensor(
+                out=gr[s][:, gs, 0:P, :].rearrange("p g r (u e) -> p g r u e", e=2),
+                in0=bank[:].bitcast(BF16).rearrange("p u g (r e) -> p g r u e", e=2),
+                in1=sc[:, gs, :].rearrange("p g (u e) -> p g u e", e=2).unsqueeze(2).to_broadcast([P, 2, P, 2, 2]),
+                op=ALU.mult,
             )
 
-        def turn(s, fill, mm):
-            b, gp = divmod(s, 2)
-            if gp == 0:
-                gr[b] = grp.tile([P, 4, 512, 4], BF16, name="gr", tag="gr", align_bytes=64)
-            g_t = gr[b]
-            g_w = g_t[:].bitcast(F32)
-            qw = [w16[s][:, c, :].bitcast(F32) for c in range(2)]
-            kw = [wkb[s][:, c, :].bitcast(F32) for c in range(2)]
-            banks = []
-            accs = []
-            for wi, words2 in enumerate((qw, kw)):
-                for g2 in range(2):
-                    bank = pst.tile([P, 2, 2, P], F32, name="tb", tag="tb")
-                    transposes(bank, words2, g2)
-                    banks.append(bank)
-                for bm in mm[wi : wi + 1]:
-                    accs.append(project(bm[0], bm[1]))
-            planes = {}
+        def scale_on_scalar(s, gh, bank):
+            planes = plp.tile([P, 2, 4, P], BF16, name="pl", tag="pl")
+            bv = bank[:].bitcast(BF16).rearrange("p u g (r e) -> p g u e r", e=2)
             for g2 in range(2):
-                g = 2 * gp + g2
-                if g2 in OFF.get(s, ()):
-                    planes[g] = plp.tile([P, 4, 256], BF16, name="pl", tag="pl")
-                    bv = banks[g2][:].bitcast(BF16).rearrange("p u c (r e) -> p u e (c r)", e=2)
-                    for t in range(4):
-                        nc.scalar.activation(
-                            out=planes[g][:, t, :], in_=bv[:, t // 2, t % 2, :], func=ACTF.Copy, scale=sc[:, g, t : t + 1]
-                        )
-                else:
-                    nc.vector.tensor_tensor(
-                        out=g_t[:, g, 0:256, :].rearrange("p r (u e) -> p r u e", e=2),
-                        in0=banks[g2][:].bitcast(BF16).rearrange("p u c (r e) -> p (c r) u e", e=2),
-                        in1=sc[:, g, :].rearrange("p (u e) -> p u e", e=2).unsqueeze(1).to_broadcast([P, 256, 2, 2]),
-                        op=ALU.mult,
+                for t in range(4):
+                    nc.scalar.activation(
+                        out=planes[:, g2, t, :], in_=bv[:, g2, t // 2, t % 2, :], func=ACTF.Copy,
+                        scale=sc[:, 2 * gh + g2, t : t + 1],
                     )
-                    for i in fill[g2 : g2 + 1]:
-                        table_step(i)
+            return planes
+
+        def interleave(s, gh, planes):
             for g2 in range(2):
-                g = 2 * gp + g2
-                nc.scalar.copy(out=g_w[:, g, 256:512, :], in_=banks[2 + g2][:].rearrange("p u c r -> p (c r) u"))
-            for g in sorted(planes):
+                if g2 in G_IL:
+                    nc.gpsimd.tensor_scalar(
+                        out=gr[s][:, 2 * gh + g2, 0:P, :], in0=planes[:, g2].rearrange("p t r -> p r t"),
+                        scalar1=1.0, scalar2=0.0, op0=ALU.mult, op1=ALU.add,
+                    )
+                    continue
                 nc.scalar.copy(
-                    out=g_t[:, g, 0:256, :].rearrange("p (c i) t -> p c t i", i=4),
-                    in_=planes[g][:].rearrange("p t (c i) -> p c t i", i=4),
+                    out=gr[s][:, 2 * gh + g2, 0:P, :].rearrange("p (c i) t -> p c t i", i=4),
+                    in_=planes[:, g2].rearrange("p t (c i) -> p c t i", i=4),
                 )
-            return accs
 
         def quant(s):
-            b, gp = divmod(s, 2)
-            if gp == 0:
-                wc[b] = wcp.tile([P, 4, 512], U32, name="wc", tag="wc", align_bytes=64)
-                ws[b] = wcp.tile([P, 4, 512], U8, name="ws", tag="ws", align_bytes=64)
-            gs = slice(2 * gp, 2 * gp + 2)
+            wc[s] = wcp.tile([P, 4, 256], U32, name="wc", tag="wc", align_bytes=64)
+            ws[s] = wcp.tile([P, 4, 256], U8, name="ws", tag="ws", align_bytes=64)
             nc.vector.quantize_mx(
-                out=wc[b][:, gs, :].rearrange("p g n -> p (g n)").bitcast(FP8X4),
-                scales=ws[b][:, gs, :].rearrange("p g n -> p (g n)"),
-                in_=gr[b][:, gs, :, :].rearrange("p g n t -> p (g n t)"),
+                out=wc[s][:].rearrange("p g n -> p (g n)").bitcast(FP8X4),
+                scales=ws[s][:].rearrange("p g n -> p (g n)"),
+                in_=gr[s][:].rearrange("p g n t -> p (g n t)"),
             )
 
-        def project(b, m):
-            acc = psa.tile([P, 512], F32, name="acc", tag="acc")
-            for g in range(4):
-                cols = slice(P * g, P * (g + 1))
-                nc.tensor.matmul_mx(
-                    out=acc[:],
-                    lhsT=xc[m][:, cols].bitcast(FP8X4),
-                    lhsT_scale=xs[m][:, cols],
-                    rhs=wc[b][:, g, :].bitcast(FP8X4),
-                    rhs_scale=ws[b][:, g, :],
-                    start=(g == 0),
-                    stop=(g == 3),
-                )
+        def project(s, pair):
+            acc = ps.tile([P, 2, 256], F32, name="acc", tag="ps")
+            for mi in range(2):
+                m = 2 * pair + mi
+                for g in range(4):
+                    cols = slice(P * g, P * (g + 1))
+                    nc.tensor.matmul_mx(
+                        out=acc[:, mi, :],
+                        lhsT=xc[m][:, cols].bitcast(FP8X4),
+                        lhsT_scale=xs[m][:, cols],
+                        rhs=wc[s][:, g, :].bitcast(FP8X4),
+                        rhs_scale=ws[s][:, g, :],
+                        start=(g == 0),
+                        stop=(g == 3),
+                    )
             return acc
 
-        def rope(b, m, acc, last):
-            a = m % 2
+        def rope(s, pair, acc, last):
             pq = rp.tile([P, 2, 4, 2, 64], F32, name="pq", tag="pq")
             nc.vector.tensor_tensor(
-                out=pq[:].rearrange("p q h w j -> p q h (w j)"),
-                in0=acc[:].rearrange("p (h d) -> p h d", d=P).unsqueeze(1).to_broadcast([P, 2, 4, P]),
-                in1=tab[:, a].rearrange("p q w j -> p q (w j)").unsqueeze(2).to_broadcast([P, 2, 4, P]),
+                out=pq[:].rearrange("p q (m h) w j -> p q m h (w j)", h=2),
+                in0=acc[:].rearrange("p m (h d) -> p m h d", d=P).unsqueeze(1).to_broadcast([P, 2, 2, 2, P]),
+                in1=tab[:].rearrange("p q a w j -> p q a (w j)").unsqueeze(3).to_broadcast([P, 2, 2, 2, P]),
                 op=ALU.mult,
             )
             adder = nc.vector if last else nc.gpsimd
             adder.tensor_tensor(out=pq[:, 0], in0=pq[:, 0], in1=pq[:, 1, :, ::-1, :], op=ALU.add)
             for o in range(2):
                 nc.sync.dma_start(
-                    out=outs[o][P * m : P * (m + 1), 256 * b : 256 * (b + 1)],
-                    in_=pq[:, 0, 2 * o : 2 * o + 2].rearrange("p h w j -> p (h w j)"),
+                    out=outs[o][256 * pair : 256 * (pair + 1), P * s : P * (s + 1)].rearrange("(m p) d -> p m d", p=P),
+                    in_=pq[:, 0].rearrange("p (m h) w j -> p m h (w j)", h=2)[:, :, o, :],
                 )
 
-        for s in range(NSTEP + LAG):
-            if s == 0:
-                for s0 in range(CAST_AHEAD):
-                    cast(s0)
-            if s == 2:
+        for i in (0, 1, 2, 3, 4):
+            table_step(i)
+        for s0 in range(CAST_AHEAD):
+            cast(s0)
+            if s0 == 0:
                 tables_finish()
-            if s < 4:
-                x_turn(s)
-            if s == 1:
-                table_step(0)
+        for s in range(NSTEP + LAG):
             j = s - LAG
-            mm = [(j // 2, 2 * (j % 2)), (j // 2, 2 * (j % 2) + 1)] if j >= 0 else []
+            accs = []
+            if s == 0:
+                x_turn(0)
+            elif s == 1:
+                x_turn(2)
+            banks = {}
             if s < NSTEP:
-                accs = turn(s, (1, 2) if s == 1 else (), mm)
-            else:
-                accs = [project(bm[0], bm[1]) for bm in mm]
-            if s < 4:
-                x_quant(s)
+                gr[s] = grp.tile([P, 4, 256, 4], BF16, name="gr", tag="gr", align_bytes=64)
+                words = w16[s][:].bitcast(F32)
+                banks = {("q", gh): turn_half(words, gh) for gh in range(2)}
+            if j >= 0:
+                accs.append(project(j, 0))
+            if s < NSTEP:
+                words = wkb[s][:].bitcast(F32)
+                for gh in range(2):
+                    banks[("k", gh)] = turn_half(words, gh)
+            if j >= 0:
+                accs.append(project(j, 1))
+            planes = {}
+            if s < NSTEP:
+                for gh in range(2):
+                    if gh in SCALAR_BANKS.get(s, ()):
+                        planes[gh] = scale_on_scalar(s, gh, banks[("q", gh)])
+                    else:
+                        scale_on_vector(s, gh, banks[("q", gh)])
+                for gh in range(2):
+                    nc.scalar.copy(
+                        out=gr[s][:].bitcast(F32)[:, 2 * gh : 2 * gh + 2, P : 2 * P, :],
+                        in_=banks[("k", gh)][:].rearrange("p u g r -> p g r u"),
+                    )
+                for gh in sorted(planes):
+                    interleave(s, gh, planes[gh])
+            if s == 0:
+                x_quant(0)
+                x_turn(1)
+            elif s == 1:
+                x_quant(1)
+                x_turn(3)
+            if 1 <= s <= NSTEP:
+                quant(s - 1)
             if s == 1:
-                table_step(3)
-                table_step(4)
+                x_quant(2)
+                x_quant(3)
             if s + CAST_AHEAD < NSTEP:
                 cast(s + CAST_AHEAD)
-            if s % 2 == 0 and 2 <= s <= NSTEP:
-                quant(s - 2)
-                quant(s - 1)
-            for bm, acc in zip(mm, accs):
-                rope(bm[0], bm[1], acc, j == NSTEP - 1 and bm[1] == 3)
+            for pair, acc in enumerate(accs):
+                rope(j, pair, acc, s == NSTEP + LAG - 1 and pair == 1)

@@ -26,6 +26,7 @@ X_ON_VECTOR = (0, 1)
 CAST_AHEAD = 2
 ROPE_BUFS = 12
 G_IL = ()
+ROPE_FIRST = True
 
 
 def tile_multiheadattention_pa_kernel(tc, x, wq_bytes, wq_scale, wk, out_0, out_1):
@@ -304,12 +305,16 @@ def tile_multiheadattention_pa_kernel(tc, x, wq_bytes, wq_scale, wk, out_0, out_
             elif s == 1:
                 x_quant(1)
                 x_turn(3)
+            if s + CAST_AHEAD < NSTEP:
+                cast(s + CAST_AHEAD)
+            if accs and ROPE_FIRST:
+                rope(j, 0, accs[0], False)
             if 1 <= s <= NSTEP:
                 quant(s - 1)
             if s == 1:
                 x_quant(2)
                 x_quant(3)
-            if s + CAST_AHEAD < NSTEP:
-                cast(s + CAST_AHEAD)
-            for pair, acc in enumerate(accs):
-                rope(j, pair, acc, s == NSTEP + LAG - 1 and pair == 1)
+            if accs:
+                if not ROPE_FIRST:
+                    rope(j, 0, accs[0], False)
+                rope(j, 1, accs[1], s == NSTEP + LAG - 1)

@@ -21,12 +21,12 @@ K = 2048
 THETA = 10000.0
 NSTEP = 16
 LAG = 2
-SCALAR_BANKS = {s: (1,) for s in range(2, 16)}
-X_ON_VECTOR = (0, 1)
+LAST_ON_V = 1
+X_ON_VECTOR = ()
+SCALAR_PASSES = {s: (2, 3) for s in range(2, 16)}
 CAST_AHEAD = 2
 ROPE_BUFS = 12
-G_IL = ()
-ROPE_FIRST = True
+G_IL = (3,)
 
 
 def tile_multiheadattention_pa_kernel(tc, x, wq_bytes, wq_scale, wk, out_0, out_1):
@@ -38,8 +38,8 @@ def tile_multiheadattention_pa_kernel(tc, x, wq_bytes, wq_scale, wk, out_0, out_
         const = ctx.enter_context(tc.tile_pool(name="const", bufs=1))
         w16p = ctx.enter_context(tc.tile_pool(name="w16p", bufs=3))
         grp = ctx.enter_context(tc.tile_pool(name="grp", bufs=3))
-        grxp = ctx.enter_context(tc.tile_pool(name="grxp", bufs=2))
-        plp = ctx.enter_context(tc.tile_pool(name="plp", bufs=3))
+        grxp = ctx.enter_context(tc.tile_pool(name="grxp", bufs=3))
+        plp = ctx.enter_context(tc.tile_pool(name="plp", bufs=6))
         wcp = ctx.enter_context(tc.tile_pool(name="wcp", bufs=3))
         rp = ctx.enter_context(tc.tile_pool(name="rp", bufs=ROPE_BUFS))
         ps = ctx.enter_context(tc.psum_pool(name="ps", bufs=8))
@@ -67,15 +67,19 @@ def tile_multiheadattention_pa_kernel(tc, x, wq_bytes, wq_scale, wk, out_0, out_
             for i in range(pieces):
                 nc.sync.dma_start(out=xr[m][:, w * i : w * (i + 1)], in_=xf[P * m : P * (m + 1), w * i : w * (i + 1)])
 
-        load_q(0)
-        load_x(0, 2)
+        for h in range(2):
+            cols = slice(K // 2 * h, K // 2 * (h + 1))
+            nc.sync.dma_start(out=wqb[0][:, cols], in_=wq_bytes[0:P, cols])
+        load_x(0, 1)
+        load_q(1)
         load_k(0)
         load_x(1, 1)
-        load_q(1)
-        load_x(2, 1)
         load_k(1)
+        load_x(2, 1)
+        load_q(2)
         load_x(3, 1)
-        for s in range(2, NSTEP):
+        load_k(2)
+        for s in range(3, NSTEP):
             load_q(s)
             load_k(s)
 
@@ -152,23 +156,28 @@ def tile_multiheadattention_pa_kernel(tc, x, wq_bytes, wq_scale, wk, out_0, out_
             xc.append(const.tile([P, 512], U32, name="xc%d" % m, align_bytes=64))
             xs.append(const.tile([P, 512], U8, name="xs%d" % m, align_bytes=64))
 
-        def turn_half(words, gh):
+        def turn(words, passes):
             bank = ps.tile([P, 2, 2, P], F32, name="tb", tag="ps")
-            for g2 in range(2):
-                g = 2 * gh + g2
+            for i, g in enumerate(passes):
                 for u in range(2):
-                    nc.tensor.transpose(bank[:, u, g2, :], words[:, 256 * g + u : 256 * (g + 1) : 2], ident[:])
+                    nc.tensor.transpose(bank[:, u, i, :], words[:, 256 * g + u : 256 * (g + 1) : 2], ident[:])
             return bank
 
-        grxs = {}
+        HALVES = ((0, 1), (2, 3))
 
-        def x_turn(m):
-            grxs[m] = grxp.tile([P, 4, P, 4], BF16, name="grx", tag="grx", align_bytes=64)
-            grx_w = grxs[m][:].bitcast(F32)
-            for gh in range(2):
-                bank = turn_half(xr[m][:].bitcast(F32), gh)
-                copier = nc.vector.tensor_copy if m in X_ON_VECTOR else nc.scalar.copy
-                copier(out=grx_w[:, 2 * gh : 2 * gh + 2, :, :], in_=bank[:].rearrange("p u g r -> p g r u"))
+        def q_groups(s):
+            mine = SCALAR_PASSES.get(s, ())
+            groups = []
+            for half in HALVES:
+                for who in (False, True):
+                    part = tuple(g for g in half if (g in mine) == who)
+                    if part:
+                        groups.append((who, part))
+            return groups
+
+        LAST0 = nc.vector if LAST_ON_V else nc.gpsimd
+        banks = {}
+        grxs = {}
 
         def x_quant(m):
             nc.vector.quantize_mx(
@@ -180,41 +189,43 @@ def tile_multiheadattention_pa_kernel(tc, x, wq_bytes, wq_scale, wk, out_0, out_
         wc = {}
         ws = {}
 
-        def cast(s):
+        def cast(s, pieces=1):
             w16[s] = w16p.tile([P, K], BF16, name="w16", tag="w16")
-            nc.scalar.copy(out=w16[s][:], in_=wqb[s][:].bitcast(FP8))
+            w = K // pieces
+            for i in range(pieces):
+                nc.scalar.copy(out=w16[s][:, w * i : w * (i + 1)], in_=wqb[s][:, w * i : w * (i + 1)].bitcast(FP8))
 
-        def scale_on_vector(s, gh, bank):
-            gs = slice(2 * gh, 2 * gh + 2)
+        def scale_on_vector(s, passes):
+            g0, n = passes[0], len(passes)
+            bank = banks["q", s, passes]
             nc.vector.tensor_tensor(
-                out=gr[s][:, gs, 0:P, :].rearrange("p g r (u e) -> p g r u e", e=2),
-                in0=bank[:].bitcast(BF16).rearrange("p u g (r e) -> p g r u e", e=2),
-                in1=sc[:, gs, :].rearrange("p g (u e) -> p g u e", e=2).unsqueeze(2).to_broadcast([P, 2, P, 2, 2]),
+                out=gr[s][:, g0 : g0 + n, 0:P, :].rearrange("p g r (u e) -> p g r u e", e=2),
+                in0=bank[:, :, 0:n, :].bitcast(BF16).rearrange("p u g (r e) -> p g r u e", e=2),
+                in1=sc[:, g0 : g0 + n, :].rearrange("p g (u e) -> p g u e", e=2).unsqueeze(2).to_broadcast([P, n, P, 2, 2]),
                 op=ALU.mult,
             )
 
-        def scale_on_scalar(s, gh, bank):
-            planes = plp.tile([P, 2, 4, P], BF16, name="pl", tag="pl")
-            bv = bank[:].bitcast(BF16).rearrange("p u g (r e) -> p g u e r", e=2)
-            for g2 in range(2):
+        def scale_on_scalar(s, passes):
+            planes = {}
+            bv = banks["q", s, passes][:].bitcast(BF16).rearrange("p u g (r e) -> p g u e r", e=2)
+            for i, g in enumerate(passes):
+                planes[g] = plp.tile([P, 4, P], BF16, name="pl", tag="pl")
                 for t in range(4):
                     nc.scalar.activation(
-                        out=planes[:, g2, t, :], in_=bv[:, g2, t // 2, t % 2, :], func=ACTF.Copy,
-                        scale=sc[:, 2 * gh + g2, t : t + 1],
+                        out=planes[g][:, t, :], in_=bv[:, i, t // 2, t % 2, :], func=ACTF.Copy, scale=sc[:, g, t : t + 1],
                     )
             return planes
 
-        def interleave(s, gh, planes):
-            for g2 in range(2):
-                if g2 in G_IL:
-                    nc.gpsimd.tensor_scalar(
-                        out=gr[s][:, 2 * gh + g2, 0:P, :], in0=planes[:, g2].rearrange("p t r -> p r t"),
-                        scalar1=1.0, scalar2=0.0, op0=ALU.mult, op1=ALU.add,
-                    )
-                    continue
+        def interleave(s, g, planes):
+            if g in G_IL:
+                nc.gpsimd.tensor_scalar(
+                    out=gr[s][:, g, 0:P, :], in0=planes[:].rearrange("p t r -> p r t"),
+                    scalar1=1.0, scalar2=0.0, op0=ALU.mult, op1=ALU.add,
+                )
+            else:
                 nc.scalar.copy(
-                    out=gr[s][:, 2 * gh + g2, 0:P, :].rearrange("p (c i) t -> p c t i", i=4),
-                    in_=planes[:, g2].rearrange("p t (c i) -> p c t i", i=4),
+                    out=gr[s][:, g, 0:P, :].rearrange("p (c i) t -> p c t i", i=4),
+                    in_=planes[:].rearrange("p t (c i) -> p c t i", i=4),
                 )
 
         def quant(s):
@@ -243,7 +254,9 @@ def tile_multiheadattention_pa_kernel(tc, x, wq_bytes, wq_scale, wk, out_0, out_
                     )
             return acc
 
-        def rope(s, pair, acc, last):
+        pqs = {}
+
+        def rope(s, pair, acc):
             pq = rp.tile([P, 2, 4, 2, 64], F32, name="pq", tag="pq")
             nc.vector.tensor_tensor(
                 out=pq[:].rearrange("p q (m h) w j -> p q m h (w j)", h=2),
@@ -251,7 +264,10 @@ def tile_multiheadattention_pa_kernel(tc, x, wq_bytes, wq_scale, wk, out_0, out_
                 in1=tab[:].rearrange("p q a w j -> p q a (w j)").unsqueeze(3).to_broadcast([P, 2, 2, 2, P]),
                 op=ALU.mult,
             )
-            adder = nc.vector if last else nc.gpsimd
+            pqs[s, pair] = pq
+
+        def finish(s, pair, adder):
+            pq = pqs[s, pair]
             adder.tensor_tensor(out=pq[:, 0], in0=pq[:, 0], in1=pq[:, 1, :, ::-1, :], op=ALU.add)
             for o in range(2):
                 nc.sync.dma_start(
@@ -259,62 +275,100 @@ def tile_multiheadattention_pa_kernel(tc, x, wq_bytes, wq_scale, wk, out_0, out_
                     in_=pq[:, 0].rearrange("p (m h) w j -> p m h (w j)", h=2)[:, :, o, :],
                 )
 
-        for i in (0, 1, 2, 3, 4):
+
+        def turn_q(s):
+            gr[s] = grp.tile([P, 4, 256, 4], BF16, name="gr", tag="gr", align_bytes=64)
+            for who, part in q_groups(s):
+                banks["q", s, part] = turn(w16[s][:].bitcast(F32), part)
+
+        def turn_k(s):
+            for gh in range(2):
+                banks["k", s, gh] = turn(wkb[s][:].bitcast(F32), HALVES[gh])
+
+        def turn_x(m):
+            grxs[m] = grxp.tile([P, 4, P, 4], BF16, name="grx", tag="grx", align_bytes=64)
+            for gh in range(2):
+                banks["x", m, gh] = turn(xr[m][:].bitcast(F32), HALVES[gh])
+
+        def copy_x(m, copier):
+            for gh in range(2):
+                copier(
+                    out=grxs[m][:].bitcast(F32)[:, 2 * gh : 2 * gh + 2, :, :],
+                    in_=banks["x", m, gh][:].rearrange("p u g r -> p g r u"),
+                )
+
+        def copy_k(s):
+            for gh in range(2):
+                nc.scalar.copy(
+                    out=gr[s][:].bitcast(F32)[:, 2 * gh : 2 * gh + 2, P : 2 * P, :],
+                    in_=banks["k", s, gh][:].rearrange("p u g r -> p g r u"),
+                )
+
+        on_vector = nc.vector.tensor_copy
+        on_scalar = nc.scalar.copy
+        XC = [on_vector if m in X_ON_VECTOR else on_scalar for m in range(4)]
+        cast(0, 2)
+        turn_q(0)
+        scale_on_vector(0, (0, 1))
+        scale_on_vector(0, (2, 3))
+        turn_x(0)
+        cast(1)
+        copy_x(0, XC[0])
+        for i in range(5):
             table_step(i)
-        for s0 in range(CAST_AHEAD):
-            cast(s0)
-            if s0 == 0:
-                tables_finish()
-        for s in range(NSTEP + LAG):
+        turn_q(1)
+        scale_on_vector(1, (0, 1))
+        scale_on_vector(1, (2, 3))
+        turn_k(0)
+        copy_k(0)
+        tables_finish()
+        turn_x(1)
+        copy_x(1, XC[1])
+        x_quant(0)
+        x_quant(1)
+        quant(0)
+        turn_k(1)
+        copy_k(1)
+        cast(2)
+        turn_x(2)
+        copy_x(2, XC[2])
+        x_quant(2)
+        turn_x(3)
+        copy_x(3, XC[3])
+        cast(3)
+        quant(1)
+        x_quant(3)
+        for s in range(2, NSTEP + LAG):
             j = s - LAG
             accs = []
-            if s == 0:
-                x_turn(0)
-            elif s == 1:
-                x_turn(2)
-            banks = {}
             if s < NSTEP:
-                gr[s] = grp.tile([P, 4, 256, 4], BF16, name="gr", tag="gr", align_bytes=64)
-                words = w16[s][:].bitcast(F32)
-                banks = {("q", gh): turn_half(words, gh) for gh in range(2)}
-            if j >= 0:
-                accs.append(project(j, 0))
+                turn_q(s)
+            accs.append(project(j, 0))
             if s < NSTEP:
-                words = wkb[s][:].bitcast(F32)
-                for gh in range(2):
-                    banks[("k", gh)] = turn_half(words, gh)
-            if j >= 0:
-                accs.append(project(j, 1))
-            planes = {}
+                turn_k(s)
+            accs.append(project(j, 1))
             if s < NSTEP:
-                for gh in range(2):
-                    if gh in SCALAR_BANKS.get(s, ()):
-                        planes[gh] = scale_on_scalar(s, gh, banks[("q", gh)])
+                planes = {}
+                for who, part in q_groups(s):
+                    if who:
+                        planes.update(scale_on_scalar(s, part))
                     else:
-                        scale_on_vector(s, gh, banks[("q", gh)])
-                for gh in range(2):
-                    nc.scalar.copy(
-                        out=gr[s][:].bitcast(F32)[:, 2 * gh : 2 * gh + 2, P : 2 * P, :],
-                        in_=banks[("k", gh)][:].rearrange("p u g r -> p g r u"),
-                    )
-                for gh in sorted(planes):
-                    interleave(s, gh, planes[gh])
-            if s == 0:
-                x_quant(0)
-                x_turn(1)
-            elif s == 1:
-                x_quant(1)
-                x_turn(3)
+                        scale_on_vector(s, part)
+                copy_k(s)
+                for g in planes:
+                    interleave(s, g, planes[g])
             if s + CAST_AHEAD < NSTEP:
                 cast(s + CAST_AHEAD)
-            if accs and ROPE_FIRST:
-                rope(j, 0, accs[0], False)
-            if 1 <= s <= NSTEP:
+            rope(j, 0, accs[0])
+            if s < NSTEP + LAG - 1:
+                finish(j, 0, nc.gpsimd)
+            if 2 < s < NSTEP:
                 quant(s - 1)
-            if s == 1:
-                x_quant(2)
-                x_quant(3)
-            if accs:
-                if not ROPE_FIRST:
-                    rope(j, 0, accs[0], False)
-                rope(j, 1, accs[1], s == NSTEP + LAG - 1)
+            if s == NSTEP - 1:
+                quant(s)
+            rope(j, 1, accs[1])
+            if s < NSTEP + LAG - 1:
+                finish(j, 1, nc.gpsimd)
+            else:
+                finish(j, 0, LAST0)
+                finish(j, 1, nc.vector)

@@ -22,10 +22,14 @@ THETA = 10000.0
 NSTEP = 16
 LAG = 2
 LAST_ON_V = 1
-X_ON_VECTOR = ()
+X_ON_VECTOR = (1,)
+TAIL = 0
+TSTEPS = 5
 SCALAR_PASSES = {s: (2, 3) for s in range(2, 16)}
 CAST_AHEAD = 2
-ROPE_BUFS = 12
+ROPE_BUFS = 5
+LOAD_AHEAD = 6
+TAILV = 1
 G_IL = (3,)
 
 
@@ -38,7 +42,7 @@ def tile_multiheadattention_pa_kernel(tc, x, wq_bytes, wq_scale, wk, out_0, out_
         const = ctx.enter_context(tc.tile_pool(name="const", bufs=1))
         w16p = ctx.enter_context(tc.tile_pool(name="w16p", bufs=3))
         grp = ctx.enter_context(tc.tile_pool(name="grp", bufs=3))
-        grxp = ctx.enter_context(tc.tile_pool(name="grxp", bufs=3))
+        grxp = ctx.enter_context(tc.tile_pool(name="grxp", bufs=2))
         plp = ctx.enter_context(tc.tile_pool(name="plp", bufs=6))
         wcp = ctx.enter_context(tc.tile_pool(name="wcp", bufs=3))
         rp = ctx.enter_context(tc.tile_pool(name="rp", bufs=ROPE_BUFS))
@@ -53,8 +57,8 @@ def tile_multiheadattention_pa_kernel(tc, x, wq_bytes, wq_scale, wk, out_0, out_
         for s in range(NSTEP):
             wqb.append(const.tile([P, K], U8, name="wqb%d" % s))
             wkb.append(const.tile([P, K], BF16, name="wkb%d" % s))
-        for m in range(4):
-            xr.append(rp.tile([P, K], BF16, name="xr%d" % m, tag="pq"))
+        for pair in range(2):
+            xr.append(rp.tile([P, 2, K], BF16, name="xr%d" % pair, tag="pq"))
 
         def load_q(s):
             nc.sync.dma_start(out=wqb[s][:], in_=wq_bytes[P * s : P * (s + 1), :])
@@ -65,7 +69,7 @@ def tile_multiheadattention_pa_kernel(tc, x, wq_bytes, wq_scale, wk, out_0, out_
         def load_x(m, pieces):
             w = K // pieces
             for i in range(pieces):
-                nc.sync.dma_start(out=xr[m][:, w * i : w * (i + 1)], in_=xf[P * m : P * (m + 1), w * i : w * (i + 1)])
+                nc.sync.dma_start(out=xr[m // 2][:, m % 2, w * i : w * (i + 1)], in_=xf[P * m : P * (m + 1), w * i : w * (i + 1)])
 
         for h in range(2):
             cols = slice(K // 2 * h, K // 2 * (h + 1))
@@ -79,7 +83,7 @@ def tile_multiheadattention_pa_kernel(tc, x, wq_bytes, wq_scale, wk, out_0, out_
         load_q(2)
         load_x(3, 1)
         load_k(2)
-        for s in range(3, NSTEP):
+        for s in range(3, LOAD_AHEAD + 2):
             load_q(s)
             load_k(s)
 
@@ -88,30 +92,28 @@ def tile_multiheadattention_pa_kernel(tc, x, wq_bytes, wq_scale, wk, out_0, out_
         warm = const.tile([P, 1], F32, name="warm")
         nc.scalar.activation(out=warm[:], in_=zero[:], func=ACTF.Sin)
 
-        ident = const.tile([P, P], F32, name="ident")
-        make_identity(nc, ident[:])
-
         pos_f = const.tile([P, 2], F32, name="pos_f")
         nc.gpsimd.iota(pos_f[:], pattern=[[P, 2]], base=0, channel_multiplier=1, allow_small_or_imprecise_dtypes=True)
+        ident = const.tile([P, P], F32, name="ident")
+        make_identity(nc, ident[:])
         freq = const.tile([P, 64], F32, name="freq")
-        nc.gpsimd.memset(freq[:, 0:1], 1.0)
+        nc.vector.memset(freq[:, 0:1], 1.0)
         w = 1
         while w < 64:
-            nc.gpsimd.tensor_scalar(
-                out=freq[:, w : 2 * w], in0=freq[:, 0:w], scalar1=THETA ** (-w / 64.0), scalar2=0.0,
-                op0=ALU.mult, op1=ALU.add,
+            nc.vector.tensor_single_scalar(
+                out=freq[:, w : 2 * w], in_=freq[:, 0:w], scalar=THETA ** (-w / 64.0), op=ALU.mult
             )
             w *= 2
         ang = const.tile([P, 2, 2, 64], F32, name="ang")
         for a in range(2):
             for f in range(2):
-                nc.gpsimd.tensor_scalar(
+                nc.vector.tensor_scalar(
                     out=ang[:, f, a, :], in0=freq[:], scalar1=pos_f[:, a : a + 1], scalar2=f * math.pi / 2.0,
                     op0=ALU.mult, op1=ALU.add,
                 )
         angf = ang[:].rearrange("p f a j -> p (f a j)")
         turns = const.tile([P, 256], F32, name="turns")
-        nc.gpsimd.tensor_scalar(out=turns[:], in0=angf, scalar1=1.0 / math.pi, scalar2=0.25, op0=ALU.mult, op1=ALU.add)
+        nc.vector.tensor_scalar(out=turns[:], in0=angf, scalar1=1.0 / math.pi, scalar2=0.25, op0=ALU.mult, op1=ALU.add)
         n_i = const.tile([P, 256], I32, name="n_i")
         red = const.tile([P, 256], F32, name="red")
         red2 = const.tile([P, 256], F32, name="red2")
@@ -152,9 +154,9 @@ def tile_multiheadattention_pa_kernel(tc, x, wq_bytes, wq_scale, wk, out_0, out_
 
         xc = []
         xs = []
-        for m in range(4):
-            xc.append(const.tile([P, 512], U32, name="xc%d" % m, align_bytes=64))
-            xs.append(const.tile([P, 512], U8, name="xs%d" % m, align_bytes=64))
+        for pair in range(2):
+            xc.append(const.tile([P, 2, 512], U32, name="xc%d" % pair, align_bytes=64))
+            xs.append(const.tile([P, 2, 512], U8, name="xs%d" % pair, align_bytes=64))
 
         def turn(words, passes):
             bank = ps.tile([P, 2, 2, P], F32, name="tb", tag="ps")
@@ -179,9 +181,11 @@ def tile_multiheadattention_pa_kernel(tc, x, wq_bytes, wq_scale, wk, out_0, out_
         banks = {}
         grxs = {}
 
-        def x_quant(m):
+        def x_quant(pair):
             nc.vector.quantize_mx(
-                out=xc[m][:].bitcast(FP8X4), scales=xs[m][:], in_=grxs[m][:].rearrange("p g r t -> p (g r t)")
+                out=xc[pair][:].rearrange("p m k -> p (m k)").bitcast(FP8X4),
+                scales=xs[pair][:].rearrange("p m k -> p (m k)"),
+                in_=grxs[pair][:].rearrange("p m g r t -> p (m g r t)"),
             )
 
         w16 = {}
@@ -240,13 +244,12 @@ def tile_multiheadattention_pa_kernel(tc, x, wq_bytes, wq_scale, wk, out_0, out_
         def project(s, pair):
             acc = ps.tile([P, 2, 256], F32, name="acc", tag="ps")
             for mi in range(2):
-                m = 2 * pair + mi
                 for g in range(4):
                     cols = slice(P * g, P * (g + 1))
                     nc.tensor.matmul_mx(
                         out=acc[:, mi, :],
-                        lhsT=xc[m][:, cols].bitcast(FP8X4),
-                        lhsT_scale=xs[m][:, cols],
+                        lhsT=xc[pair][:, mi, cols].bitcast(FP8X4),
+                        lhsT_scale=xs[pair][:, mi, cols],
                         rhs=wc[s][:, g, :].bitcast(FP8X4),
                         rhs_scale=ws[s][:, g, :],
                         start=(g == 0),
@@ -257,23 +260,30 @@ def tile_multiheadattention_pa_kernel(tc, x, wq_bytes, wq_scale, wk, out_0, out_
         pqs = {}
 
         def rope(s, pair, acc):
-            pq = rp.tile([P, 2, 4, 2, 64], F32, name="pq", tag="pq")
+            n = 2 * s + pair
+            if n == 0 or n % 2 == 1:
+                pqs[(n + 1) // 2] = rp.tile([P, 2, 2, 4, 2, 64], F32, name="pq", tag="pq")
+            pq = pqs[(n + 1) // 2]
             nc.vector.tensor_tensor(
-                out=pq[:].rearrange("p q (m h) w j -> p q m h (w j)", h=2),
+                out=pq[:, :, (n + 1) % 2].rearrange("p q (m h) w j -> p q m h (w j)", h=2),
                 in0=acc[:].rearrange("p m (h d) -> p m h d", d=P).unsqueeze(1).to_broadcast([P, 2, 2, 2, P]),
                 in1=tab[:].rearrange("p q a w j -> p q a (w j)").unsqueeze(3).to_broadcast([P, 2, 2, 2, P]),
                 op=ALU.mult,
             )
-            pqs[s, pair] = pq
 
-        def finish(s, pair, adder):
-            pq = pqs[s, pair]
-            adder.tensor_tensor(out=pq[:, 0], in0=pq[:, 0], in1=pq[:, 1, :, ::-1, :], op=ALU.add)
-            for o in range(2):
-                nc.sync.dma_start(
-                    out=outs[o][256 * pair : 256 * (pair + 1), P * s : P * (s + 1)].rearrange("(m p) d -> p m d", p=P),
-                    in_=pq[:, 0].rearrange("p (m h) w j -> p m h (w j)", h=2)[:, :, o, :],
-                )
+        def finish(first, last, adder):
+            pq = pqs[(first + 1) // 2]
+            i0, i1 = (first + 1) % 2, (last + 1) % 2 + 1
+            adder.tensor_tensor(
+                out=pq[:, 0, i0:i1], in0=pq[:, 0, i0:i1], in1=pq[:, 1, i0:i1, :, ::-1, :], op=ALU.add
+            )
+            for n in range(first, last + 1):
+                s, pair = divmod(n, 2)
+                for o in range(2):
+                    nc.sync.dma_start(
+                        out=outs[o][256 * pair : 256 * (pair + 1), P * s : P * (s + 1)].rearrange("(m p) d -> p m d", p=P),
+                        in_=pq[:, 0, (n + 1) % 2].rearrange("p (m h) w j -> p m h (w j)", h=2)[:, :, o, :],
+                    )
 
 
         def turn_q(s):
@@ -286,14 +296,15 @@ def tile_multiheadattention_pa_kernel(tc, x, wq_bytes, wq_scale, wk, out_0, out_
                 banks["k", s, gh] = turn(wkb[s][:].bitcast(F32), HALVES[gh])
 
         def turn_x(m):
-            grxs[m] = grxp.tile([P, 4, P, 4], BF16, name="grx", tag="grx", align_bytes=64)
+            if m % 2 == 0:
+                grxs[m // 2] = grxp.tile([P, 2, 4, P, 4], BF16, name="grx", tag="grx", align_bytes=64)
             for gh in range(2):
-                banks["x", m, gh] = turn(xr[m][:].bitcast(F32), HALVES[gh])
+                banks["x", m, gh] = turn(xr[m // 2][:, m % 2, :].bitcast(F32), HALVES[gh])
 
         def copy_x(m, copier):
             for gh in range(2):
                 copier(
-                    out=grxs[m][:].bitcast(F32)[:, 2 * gh : 2 * gh + 2, :, :],
+                    out=grxs[m // 2][:].bitcast(F32)[:, m % 2, 2 * gh : 2 * gh + 2, :, :],
                     in_=banks["x", m, gh][:].rearrange("p u g r -> p g r u"),
                 )
 
@@ -307,15 +318,17 @@ def tile_multiheadattention_pa_kernel(tc, x, wq_bytes, wq_scale, wk, out_0, out_
         on_vector = nc.vector.tensor_copy
         on_scalar = nc.scalar.copy
         XC = [on_vector if m in X_ON_VECTOR else on_scalar for m in range(4)]
+        for i in range(TSTEPS):
+            table_step(i)
         cast(0, 2)
         turn_q(0)
         scale_on_vector(0, (0, 1))
         scale_on_vector(0, (2, 3))
+        for i in range(TSTEPS, 5):
+            table_step(i)
         turn_x(0)
         cast(1)
         copy_x(0, XC[0])
-        for i in range(5):
-            table_step(i)
         turn_q(1)
         scale_on_vector(1, (0, 1))
         scale_on_vector(1, (2, 3))
@@ -325,22 +338,23 @@ def tile_multiheadattention_pa_kernel(tc, x, wq_bytes, wq_scale, wk, out_0, out_
         turn_x(1)
         copy_x(1, XC[1])
         x_quant(0)
-        x_quant(1)
         quant(0)
+        cast(2)
         turn_k(1)
         copy_k(1)
-        cast(2)
+        quant(1)
         turn_x(2)
         copy_x(2, XC[2])
-        x_quant(2)
         turn_x(3)
         copy_x(3, XC[3])
         cast(3)
-        quant(1)
-        x_quant(3)
+        x_quant(1)
         for s in range(2, NSTEP + LAG):
             j = s - LAG
             accs = []
+            if s + LOAD_AHEAD < NSTEP:
+                load_q(s + LOAD_AHEAD)
+                load_k(s + LOAD_AHEAD)
             if s < NSTEP:
                 turn_q(s)
             accs.append(project(j, 0))
@@ -360,15 +374,21 @@ def tile_multiheadattention_pa_kernel(tc, x, wq_bytes, wq_scale, wk, out_0, out_
             if s + CAST_AHEAD < NSTEP:
                 cast(s + CAST_AHEAD)
             rope(j, 0, accs[0])
-            if s < NSTEP + LAG - 1:
-                finish(j, 0, nc.gpsimd)
+            if j == 0:
+                finish(0, 0, nc.gpsimd)
+            elif j < NSTEP - TAILV:
+                finish(2 * j - 1, 2 * j, nc.gpsimd)
+            else:
+                finish(2 * j - 1, 2 * j - 1, nc.gpsimd)
+                if j < NSTEP - 1:
+                    finish(2 * j, 2 * j, nc.gpsimd)
             if 2 < s < NSTEP:
                 quant(s - 1)
-            if s == NSTEP - 1:
+            if s == NSTEP - 1 and not TAIL:
                 quant(s)
             rope(j, 1, accs[1])
-            if s < NSTEP + LAG - 1:
-                finish(j, 1, nc.gpsimd)
-            else:
-                finish(j, 0, LAST0)
-                finish(j, 1, nc.vector)
+            if s == NSTEP - 1 and TAIL:
+                quant(s)
+            if j == NSTEP - 1:
+                finish(2 * j, 2 * j, nc.vector)
+                finish(2 * j + 1, 2 * j + 1, nc.vector)

@@ -22,9 +22,8 @@ THETA = 10000.0
 NSTEP = 16
 LAG = 2
 LAST_ON_V = 1
-X_ON_VECTOR = (1,)
+X_ON_VECTOR = ()
 TAIL = 0
-TSTEPS = 5
 SCALAR_PASSES = {s: (2, 3) for s in range(2, 16)}
 CAST_AHEAD = 2
 ROPE_BUFS = 5
@@ -76,8 +75,8 @@ def tile_multiheadattention_pa_kernel(tc, x, wq_bytes, wq_scale, wk, out_0, out_
             nc.sync.dma_start(out=wqb[0][:, cols], in_=wq_bytes[0:P, cols])
         load_x(0, 1)
         load_q(1)
-        load_k(0)
         load_x(1, 1)
+        load_k(0)
         load_k(1)
         load_x(2, 1)
         load_q(2)
@@ -97,60 +96,41 @@ def tile_multiheadattention_pa_kernel(tc, x, wq_bytes, wq_scale, wk, out_0, out_
         ident = const.tile([P, P], F32, name="ident")
         make_identity(nc, ident[:])
         freq = const.tile([P, 64], F32, name="freq")
-        nc.vector.memset(freq[:, 0:1], 1.0)
+        nc.gpsimd.memset(freq[:, 0:1], 1.0)
         w = 1
         while w < 64:
-            nc.vector.tensor_single_scalar(
-                out=freq[:, w : 2 * w], in_=freq[:, 0:w], scalar=THETA ** (-w / 64.0), op=ALU.mult
+            nc.gpsimd.tensor_scalar(
+                out=freq[:, w : 2 * w], in0=freq[:, 0:w], scalar1=THETA ** (-w / 64.0), scalar2=0.0,
+                op0=ALU.mult, op1=ALU.add,
             )
             w *= 2
         ang = const.tile([P, 2, 2, 64], F32, name="ang")
         for a in range(2):
             for f in range(2):
-                nc.vector.tensor_scalar(
+                nc.gpsimd.tensor_scalar(
                     out=ang[:, f, a, :], in0=freq[:], scalar1=pos_f[:, a : a + 1], scalar2=f * math.pi / 2.0,
                     op0=ALU.mult, op1=ALU.add,
                 )
         angf = ang[:].rearrange("p f a j -> p (f a j)")
-        turns = const.tile([P, 256], F32, name="turns")
-        nc.vector.tensor_scalar(out=turns[:], in0=angf, scalar1=1.0 / math.pi, scalar2=0.25, op0=ALU.mult, op1=ALU.add)
         n_i = const.tile([P, 256], I32, name="n_i")
         red = const.tile([P, 256], F32, name="red")
-        red2 = const.tile([P, 256], F32, name="red2")
-        par = const.tile([P, 256], I32, name="par")
-        sgn = const.tile([P, 2, 2, 64], F32, name="sgn")
         sn = const.tile([P, 2, 2, 64], F32, name="sn")
         tab = const.tile([P, 2, 2, 2, 64], F32, name="tab")
-        pi_hi = math.floor(math.pi * 16384.0) / 16384.0
-        pi_lo = math.pi - pi_hi
 
         def table_step(i):
             if i == 0:
-                nc.vector.tensor_copy(out=n_i[:], in_=turns[:])
-            elif i == 1:
-                nc.vector.tensor_single_scalar(out=par[:], in_=n_i[:], scalar=1, op=ALU.bitwise_and)
-            elif i == 2:
-                nc.vector.scalar_tensor_tensor(
-                    out=red[:], in0=n_i[:], scalar=-pi_hi, in1=angf, op0=ALU.mult, op1=ALU.add
-                )
-            elif i == 3:
-                nc.vector.tensor_scalar(
-                    out=sgn[:].rearrange("p f a j -> p (f a j)"), in0=par[:], scalar1=-2.0, scalar2=1.0,
-                    op0=ALU.mult, op1=ALU.add,
-                )
+                nc.vector.tensor_scalar(out=n_i[:], in0=angf, scalar1=0.5 / math.pi, scalar2=None, op0=ALU.mult)
             else:
                 nc.vector.scalar_tensor_tensor(
-                    out=red2[:], in0=n_i[:], scalar=-pi_lo, in1=red[:], op0=ALU.mult, op1=ALU.add
+                    out=red[:], in0=n_i[:], scalar=-2.0 * math.pi, in1=angf, op0=ALU.mult, op1=ALU.add
                 )
 
         def tables_finish():
-            nc.scalar.activation(out=sn[:].rearrange("p f a j -> p (f a j)"), in_=red2[:], func=ACTF.Sin)
-            for wv in range(2):
-                nc.gpsimd.tensor_tensor(out=tab[:, 0, :, wv, :], in0=sn[:, 1], in1=sgn[:, 1], op=ALU.mult)
-            nc.gpsimd.tensor_tensor(out=tab[:, 1, :, 0, :], in0=sn[:, 0], in1=sgn[:, 0], op=ALU.mult)
-            nc.gpsimd.tensor_scalar(
-                out=tab[:, 1, :, 1, :], in0=tab[:, 1, :, 0, :], scalar1=-1.0, scalar2=0.0, op0=ALU.mult, op1=ALU.add
-            )
+            nc.scalar.activation(out=sn[:].rearrange("p f a j -> p (f a j)"), in_=red[:], func=ACTF.Sin)
+            for q, wv, f, sign in ((0, 0, 1, 1.0), (0, 1, 1, 1.0), (1, 0, 0, 1.0), (1, 1, 0, -1.0)):
+                nc.gpsimd.tensor_scalar(
+                    out=tab[:, q, :, wv, :], in0=sn[:, f], scalar1=sign, scalar2=0.0, op0=ALU.mult, op1=ALU.add
+                )
 
         xc = []
         xs = []
@@ -318,26 +298,24 @@ def tile_multiheadattention_pa_kernel(tc, x, wq_bytes, wq_scale, wk, out_0, out_
         on_vector = nc.vector.tensor_copy
         on_scalar = nc.scalar.copy
         XC = [on_vector if m in X_ON_VECTOR else on_scalar for m in range(4)]
-        for i in range(TSTEPS):
-            table_step(i)
         cast(0, 2)
         turn_q(0)
         scale_on_vector(0, (0, 1))
+        table_step(0)
         scale_on_vector(0, (2, 3))
-        for i in range(TSTEPS, 5):
-            table_step(i)
+        table_step(1)
         turn_x(0)
         cast(1)
         copy_x(0, XC[0])
         turn_q(1)
         scale_on_vector(1, (0, 1))
         scale_on_vector(1, (2, 3))
-        turn_k(0)
-        copy_k(0)
-        tables_finish()
         turn_x(1)
         copy_x(1, XC[1])
         x_quant(0)
+        turn_k(0)
+        tables_finish()
+        copy_k(0)
         quant(0)
         cast(2)
         turn_k(1)

@@ -23,13 +23,12 @@ NSTEP = 16
 LAG = 2
 LAST_ON_V = 1
 X_ON_VECTOR = ()
-TAIL = 0
-SCALAR_PASSES = {s: (2, 3) for s in range(2, 16)}
+SCALAR_PASSES = {s: (2, 3) if s < 15 else (3,) for s in range(2, 16)}
 CAST_AHEAD = 2
-ROPE_BUFS = 5
+ROPE_BUFS = 10
 LOAD_AHEAD = 6
-TAILV = 1
 G_IL = (3,)
+IL_ROWS = 64
 
 
 def tile_multiheadattention_pa_kernel(tc, x, wq_bytes, wq_scale, wk, out_0, out_1):
@@ -56,8 +55,8 @@ def tile_multiheadattention_pa_kernel(tc, x, wq_bytes, wq_scale, wk, out_0, out_
         for s in range(NSTEP):
             wqb.append(const.tile([P, K], U8, name="wqb%d" % s))
             wkb.append(const.tile([P, K], BF16, name="wkb%d" % s))
-        for pair in range(2):
-            xr.append(rp.tile([P, 2, K], BF16, name="xr%d" % pair, tag="pq"))
+        for m in range(4):
+            xr.append(rp.tile([P, K], BF16, name="xr%d" % m, tag="pq"))
 
         def load_q(s):
             nc.sync.dma_start(out=wqb[s][:], in_=wq_bytes[P * s : P * (s + 1), :])
@@ -68,7 +67,7 @@ def tile_multiheadattention_pa_kernel(tc, x, wq_bytes, wq_scale, wk, out_0, out_
         def load_x(m, pieces):
             w = K // pieces
             for i in range(pieces):
-                nc.sync.dma_start(out=xr[m // 2][:, m % 2, w * i : w * (i + 1)], in_=xf[P * m : P * (m + 1), w * i : w * (i + 1)])
+                nc.sync.dma_start(out=xr[m][:, w * i : w * (i + 1)], in_=xf[P * m : P * (m + 1), w * i : w * (i + 1)])
 
         for h in range(2):
             cols = slice(K // 2 * h, K // 2 * (h + 1))
@@ -201,15 +200,16 @@ def tile_multiheadattention_pa_kernel(tc, x, wq_bytes, wq_scale, wk, out_0, out_
             return planes
 
         def interleave(s, g, planes):
-            if g in G_IL:
+            rows = IL_ROWS if g in G_IL else 0
+            if rows:
                 nc.gpsimd.tensor_scalar(
-                    out=gr[s][:, g, 0:P, :], in0=planes[:].rearrange("p t r -> p r t"),
+                    out=gr[s][:, g, 0:rows, :], in0=planes[:, :, 0:rows].rearrange("p t r -> p r t"),
                     scalar1=1.0, scalar2=0.0, op0=ALU.mult, op1=ALU.add,
                 )
-            else:
+            if rows < P:
                 nc.scalar.copy(
-                    out=gr[s][:, g, 0:P, :].rearrange("p (c i) t -> p c t i", i=4),
-                    in_=planes[:].rearrange("p t (c i) -> p c t i", i=4),
+                    out=gr[s][:, g, rows:P, :].rearrange("p (c i) t -> p c t i", i=4),
+                    in_=planes[:, :, rows:P].rearrange("p t (c i) -> p c t i", i=4),
                 )
 
         def quant(s):
@@ -240,30 +240,23 @@ def tile_multiheadattention_pa_kernel(tc, x, wq_bytes, wq_scale, wk, out_0, out_
         pqs = {}
 
         def rope(s, pair, acc):
-            n = 2 * s + pair
-            if n == 0 or n % 2 == 1:
-                pqs[(n + 1) // 2] = rp.tile([P, 2, 2, 4, 2, 64], F32, name="pq", tag="pq")
-            pq = pqs[(n + 1) // 2]
+            pq = rp.tile([P, 2, 4, 2, 64], F32, name="pq", tag="pq")
             nc.vector.tensor_tensor(
-                out=pq[:, :, (n + 1) % 2].rearrange("p q (m h) w j -> p q m h (w j)", h=2),
+                out=pq[:].rearrange("p q (m h) w j -> p q m h (w j)", h=2),
                 in0=acc[:].rearrange("p m (h d) -> p m h d", d=P).unsqueeze(1).to_broadcast([P, 2, 2, 2, P]),
                 in1=tab[:].rearrange("p q a w j -> p q a (w j)").unsqueeze(3).to_broadcast([P, 2, 2, 2, P]),
                 op=ALU.mult,
             )
+            pqs[s, pair] = pq
 
-        def finish(first, last, adder):
-            pq = pqs[(first + 1) // 2]
-            i0, i1 = (first + 1) % 2, (last + 1) % 2 + 1
-            adder.tensor_tensor(
-                out=pq[:, 0, i0:i1], in0=pq[:, 0, i0:i1], in1=pq[:, 1, i0:i1, :, ::-1, :], op=ALU.add
-            )
-            for n in range(first, last + 1):
-                s, pair = divmod(n, 2)
-                for o in range(2):
-                    nc.sync.dma_start(
-                        out=outs[o][256 * pair : 256 * (pair + 1), P * s : P * (s + 1)].rearrange("(m p) d -> p m d", p=P),
-                        in_=pq[:, 0, (n + 1) % 2].rearrange("p (m h) w j -> p m h (w j)", h=2)[:, :, o, :],
-                    )
+        def finish(s, pair, adder):
+            pq = pqs[s, pair]
+            adder.tensor_tensor(out=pq[:, 0], in0=pq[:, 0], in1=pq[:, 1, :, ::-1, :], op=ALU.add)
+            for o in range(2):
+                nc.sync.dma_start(
+                    out=outs[o][256 * pair : 256 * (pair + 1), P * s : P * (s + 1)].rearrange("(m p) d -> p m d", p=P),
+                    in_=pq[:, 0].rearrange("p (m h) w j -> p m h (w j)", h=2)[:, :, o, :],
+                )
 
 
         def turn_q(s):
@@ -279,7 +272,7 @@ def tile_multiheadattention_pa_kernel(tc, x, wq_bytes, wq_scale, wk, out_0, out_
             if m % 2 == 0:
                 grxs[m // 2] = grxp.tile([P, 2, 4, P, 4], BF16, name="grx", tag="grx", align_bytes=64)
             for gh in range(2):
-                banks["x", m, gh] = turn(xr[m // 2][:, m % 2, :].bitcast(F32), HALVES[gh])
+                banks["x", m, gh] = turn(xr[m][:].bitcast(F32), HALVES[gh])
 
         def copy_x(m, copier):
             for gh in range(2):
@@ -352,21 +345,15 @@ def tile_multiheadattention_pa_kernel(tc, x, wq_bytes, wq_scale, wk, out_0, out_
             if s + CAST_AHEAD < NSTEP:
                 cast(s + CAST_AHEAD)
             rope(j, 0, accs[0])
-            if j == 0:
-                finish(0, 0, nc.gpsimd)
-            elif j < NSTEP - TAILV:
-                finish(2 * j - 1, 2 * j, nc.gpsimd)
-            else:
-                finish(2 * j - 1, 2 * j - 1, nc.gpsimd)
-                if j < NSTEP - 1:
-                    finish(2 * j, 2 * j, nc.gpsimd)
+            if j < NSTEP - 1:
+                finish(j, 0, nc.gpsimd)
             if 2 < s < NSTEP:
                 quant(s - 1)
-            if s == NSTEP - 1 and not TAIL:
+            if s == NSTEP - 1:
                 quant(s)
             rope(j, 1, accs[1])
-            if s == NSTEP - 1 and TAIL:
-                quant(s)
-            if j == NSTEP - 1:
-                finish(2 * j, 2 * j, nc.vector)
-                finish(2 * j + 1, 2 * j + 1, nc.vector)
+            if j < NSTEP - 1:
+                finish(j, 1, nc.gpsimd)
+            else:
+                finish(j, 0, nc.vector)
+                finish(j, 1, nc.vector)

@@ -313,9 +313,9 @@ def tile_multiheadattention_pa_kernel(tc, x, wq_bytes, wq_scale, wk, out_0, out_
         cast(2)
         turn_k(1)
         copy_k(1)
-        quant(1)
         turn_x(2)
-        copy_x(2, XC[2])
+        copy_x(2, on_vector)
+        quant(1)
         turn_x(3)
         copy_x(3, XC[3])
         cast(3)

@@ -53,10 +53,10 @@ def tile_multiheadattention_pa_kernel(tc, x, wq_bytes, wq_scale, wk, out_0, out_
         wkb = []
         xr = []
         for s in range(NSTEP):
-            wqb.append(const.tile([P, K], U8, name="wqb%d" % s))
-            wkb.append(const.tile([P, K], BF16, name="wkb%d" % s))
+            wqb.append(const.tile([P, K], U8, name="wqb%d" % s, align_bytes=256))
+            wkb.append(const.tile([P, K], BF16, name="wkb%d" % s, align_bytes=256))
         for m in range(4):
-            xr.append(rp.tile([P, K], BF16, name="xr%d" % m, tag="pq"))
+            xr.append(rp.tile([P, K], BF16, name="xr%d" % m, tag="pq", align_bytes=256))
 
         def load_q(s):
             nc.sync.dma_start(out=wqb[s][:], in_=wq_bytes[P * s : P * (s + 1), :])
@@ -92,7 +92,7 @@ def tile_multiheadattention_pa_kernel(tc, x, wq_bytes, wq_scale, wk, out_0, out_
 
         pos_f = const.tile([P, 2], F32, name="pos_f")
         nc.gpsimd.iota(pos_f[:], pattern=[[P, 2]], base=0, channel_multiplier=1, allow_small_or_imprecise_dtypes=True)
-        ident = const.tile([P, P], F32, name="ident")
+        ident = const.tile([P, P], F32, name="ident", align_bytes=256)
         make_identity(nc, ident[:])
         freq = const.tile([P, 64], F32, name="freq")
         nc.gpsimd.memset(freq[:, 0:1], 1.0)
@@ -114,7 +114,7 @@ def tile_multiheadattention_pa_kernel(tc, x, wq_bytes, wq_scale, wk, out_0, out_
         n_i = const.tile([P, 256], I32, name="n_i")
         red = const.tile([P, 256], F32, name="red")
         sn = const.tile([P, 2, 2, 64], F32, name="sn")
-        tab = const.tile([P, 2, 2, 2, 64], F32, name="tab")
+        tab = const.tile([P, 2, 2, 2, 64], F32, name="tab", align_bytes=256)
 
         def table_step(i):
             if i == 0:
@@ -134,8 +134,8 @@ def tile_multiheadattention_pa_kernel(tc, x, wq_bytes, wq_scale, wk, out_0, out_
         xc = []
         xs = []
         for pair in range(2):
-            xc.append(const.tile([P, 2, 512], U32, name="xc%d" % pair, align_bytes=64))
-            xs.append(const.tile([P, 2, 512], U8, name="xs%d" % pair, align_bytes=64))
+            xc.append(const.tile([P, 2, 512], U32, name="xc%d" % pair, align_bytes=256))
+            xs.append(const.tile([P, 2, 512], U8, name="xs%d" % pair, align_bytes=256))
 
         def turn(words, passes):
             bank = ps.tile([P, 2, 2, P], F32, name="tb", tag="ps")
@@ -173,7 +173,7 @@ def tile_multiheadattention_pa_kernel(tc, x, wq_bytes, wq_scale, wk, out_0, out_
         ws = {}
 
         def cast(s, pieces=1):
-            w16[s] = w16p.tile([P, K], BF16, name="w16", tag="w16")
+            w16[s] = w16p.tile([P, K], BF16, name="w16", tag="w16", align_bytes=256)
             w = K // pieces
             for i in range(pieces):
                 nc.scalar.copy(out=w16[s][:, w * i : w * (i + 1)], in_=wqb[s][:, w * i : w * (i + 1)].bitcast(FP8))
@@ -192,7 +192,7 @@ def tile_multiheadattention_pa_kernel(tc, x, wq_bytes, wq_scale, wk, out_0, out_
             planes = {}
             bv = banks["q", s, passes][:].bitcast(BF16).rearrange("p u g (r e) -> p g u e r", e=2)
             for i, g in enumerate(passes):
-                planes[g] = plp.tile([P, 4, P], BF16, name="pl", tag="pl")
+                planes[g] = plp.tile([P, 4, P], BF16, name="pl", tag="pl", align_bytes=256)
                 for t in range(4):
                     nc.scalar.activation(
                         out=planes[g][:, t, :], in_=bv[:, i, t // 2, t % 2, :], func=ACTF.Copy, scale=sc[:, g, t : t + 1],
@@ -213,8 +213,8 @@ def tile_multiheadattention_pa_kernel(tc, x, wq_bytes, wq_scale, wk, out_0, out_
                 )
 
         def quant(s):
-            wc[s] = wcp.tile([P, 4, 256], U32, name="wc", tag="wc", align_bytes=64)
-            ws[s] = wcp.tile([P, 4, 256], U8, name="ws", tag="ws", align_bytes=64)
+            wc[s] = wcp.tile([P, 4, 256], U32, name="wc", tag="wc", align_bytes=256)
+            ws[s] = wcp.tile([P, 4, 256], U8, name="ws", tag="ws", align_bytes=256)
             nc.vector.quantize_mx(
                 out=wc[s][:].rearrange("p g n -> p (g n)").bitcast(FP8X4),
                 scales=ws[s][:].rearrange("p g n -> p (g n)"),
@@ -240,7 +240,7 @@ def tile_multiheadattention_pa_kernel(tc, x, wq_bytes, wq_scale, wk, out_0, out_
         pqs = {}
 
         def rope(s, pair, acc):
-            pq = rp.tile([P, 2, 4, 2, 64], F32, name="pq", tag="pq")
+            pq = rp.tile([P, 2, 4, 2, 64], F32, name="pq", tag="pq", align_bytes=256)
             nc.vector.tensor_tensor(
                 out=pq[:].rearrange("p q (m h) w j -> p q m h (w j)", h=2),
                 in0=acc[:].rearrange("p m (h d) -> p m h d", d=P).unsqueeze(1).to_broadcast([P, 2, 2, 2, P]),
@@ -260,7 +260,7 @@ def tile_multiheadattention_pa_kernel(tc, x, wq_bytes, wq_scale, wk, out_0, out_
 
 
         def turn_q(s):
-            gr[s] = grp.tile([P, 4, 256, 4], BF16, name="gr", tag="gr", align_bytes=64)
+            gr[s] = grp.tile([P, 4, 256, 4], BF16, name="gr", tag="gr", align_bytes=256)
             for who, part in q_groups(s):
                 banks["q", s, part] = turn(w16[s][:].bitcast(F32), part)
 
@@ -270,7 +270,7 @@ def tile_multiheadattention_pa_kernel(tc, x, wq_bytes, wq_scale, wk, out_0, out_
 
         def turn_x(m):
             if m % 2 == 0:
-                grxs[m // 2] = grxp.tile([P, 2, 4, P, 4], BF16, name="grx", tag="grx", align_bytes=64)
+                grxs[m // 2] = grxp.tile([P, 2, 4, P, 4], BF16, name="grx", tag="grx", align_bytes=256)
             for gh in range(2):
                 banks["x", m, gh] = turn(xr[m][:].bitcast(F32), HALVES[gh])
 

from contextlib import ExitStack
import math

import concourse.mybir as mybir
from concourse.masks import make_identity

FLOPS = 2 * 512 * 2048 * 4096

F32 = mybir.dt.float32
BF16 = mybir.dt.bfloat16
U32 = mybir.dt.uint32
U8 = mybir.dt.uint8
I32 = mybir.dt.int32
FP8 = mybir.dt.float8_e4m3fn
FP8X4 = mybir.dt.float8_e4m3fn_x4
ALU = mybir.AluOpType
ACTF = mybir.ActivationFunctionType

P = 128
K = 2048
THETA = 10000.0
NSTEP = 16
LAG = 2
LAST_ON_V = 1
X_ON_VECTOR = ()
SCALAR_PASSES = {s: (2, 3) if s < 15 else (3,) for s in range(2, 16)}
CAST_AHEAD = 2
ROPE_BUFS = 10
LOAD_AHEAD = 6
G_IL = (3,)
IL_ROWS = 64


def tile_multiheadattention_pa_kernel(tc, x, wq_bytes, wq_scale, wk, out_0, out_1):
    nc = tc.nc
    xf = x.flatten_outer_dims()
    outs = (out_0.rearrange("b s h d -> (b s) (h d)"), out_1.rearrange("b s h d -> (b s) (h d)"))

    with ExitStack() as ctx:
        const = ctx.enter_context(tc.tile_pool(name="const", bufs=1))
        w16p = ctx.enter_context(tc.tile_pool(name="w16p", bufs=3))
        grp = ctx.enter_context(tc.tile_pool(name="grp", bufs=3))
        grxp = ctx.enter_context(tc.tile_pool(name="grxp", bufs=2))
        plp = ctx.enter_context(tc.tile_pool(name="plp", bufs=6))
        wcp = ctx.enter_context(tc.tile_pool(name="wcp", bufs=3))
        rp = ctx.enter_context(tc.tile_pool(name="rp", bufs=ROPE_BUFS))
        ps = ctx.enter_context(tc.psum_pool(name="ps", bufs=8))
        ctx.enter_context(tc.manual_schedule())

        sc = const.tile([P, 4, 4], F32, name="sc")
        nc.scalar.dma_start(out=sc[:], in_=wq_scale.rearrange("o (g p t) -> p (o g) t", p=P, t=4))
        wqb = []
        wkb = []
        xr = []
        for s in range(NSTEP):
            wqb.append(const.tile([P, K], U8, name="wqb%d" % s, align_bytes=256))
            wkb.append(const.tile([P, K], BF16, name="wkb%d" % s, align_bytes=256))
        for m in range(4):
            xr.append(rp.tile([P, K], BF16, name="xr%d" % m, tag="pq", align_bytes=256))

        def load_q(s):
            nc.sync.dma_start(out=wqb[s][:], in_=wq_bytes[P * s : P * (s + 1), :])

        def load_k(s):
            nc.sync.dma_start(out=wkb[s][:], in_=wk[P * s : P * (s + 1), :])

        def load_x(m, pieces):
            w = K // pieces
            for i in range(pieces):
                nc.sync.dma_start(out=xr[m][:, w * i : w * (i + 1)], in_=xf[P * m : P * (m + 1), w * i : w * (i + 1)])

        for h in range(2):
            cols = slice(K // 2 * h, K // 2 * (h + 1))
            nc.sync.dma_start(out=wqb[0][:, cols], in_=wq_bytes[0:P, cols])
        load_x(0, 1)
        load_q(1)
        load_x(1, 1)
        load_k(0)
        load_k(1)
        load_x(2, 1)
        load_q(2)
        load_x(3, 1)
        load_k(2)
        for s in range(3, LOAD_AHEAD + 2):
            load_q(s)
            load_k(s)

        zero = const.tile([P, 1], F32, name="zero")
        nc.vector.memset(zero[:], 0.0)
        warm = const.tile([P, 1], F32, name="warm")
        nc.scalar.activation(out=warm[:], in_=zero[:], func=ACTF.Sin)

        pos_f = const.tile([P, 2], F32, name="pos_f")
        nc.gpsimd.iota(pos_f[:], pattern=[[P, 2]], base=0, channel_multiplier=1, allow_small_or_imprecise_dtypes=True)
        ident = const.tile([P, P], F32, name="ident", align_bytes=256)
        make_identity(nc, ident[:])
        freq = const.tile([P, 64], F32, name="freq")
        nc.gpsimd.memset(freq[:, 0:1], 1.0)
        w = 1
        while w < 64:
            nc.gpsimd.tensor_scalar(
                out=freq[:, w : 2 * w], in0=freq[:, 0:w], scalar1=THETA ** (-w / 64.0), scalar2=0.0,
                op0=ALU.mult, op1=ALU.add,
            )
            w *= 2
        ang = const.tile([P, 2, 2, 64], F32, name="ang")
        for a in range(2):
            for f in range(2):
                nc.gpsimd.tensor_scalar(
                    out=ang[:, f, a, :], in0=freq[:], scalar1=pos_f[:, a : a + 1], scalar2=f * math.pi / 2.0,
                    op0=ALU.mult, op1=ALU.add,
                )
        angf = ang[:].rearrange("p f a j -> p (f a j)")
        n_i = const.tile([P, 256], I32, name="n_i")
        red = const.tile([P, 256], F32, name="red")
        sn = const.tile([P, 2, 2, 64], F32, name="sn")
        tab = const.tile([P, 2, 2, 2, 64], F32, name="tab", align_bytes=256)

        def table_step(i):
            if i == 0:
                nc.vector.tensor_scalar(out=n_i[:], in0=angf, scalar1=0.5 / math.pi, scalar2=None, op0=ALU.mult)
            else:
                nc.vector.scalar_tensor_tensor(
                    out=red[:], in0=n_i[:], scalar=-2.0 * math.pi, in1=angf, op0=ALU.mult, op1=ALU.add
                )

        def tables_finish():
            nc.scalar.activation(out=sn[:].rearrange("p f a j -> p (f a j)"), in_=red[:], func=ACTF.Sin)
            for q, wv, f, sign in ((0, 0, 1, 1.0), (0, 1, 1, 1.0), (1, 0, 0, 1.0), (1, 1, 0, -1.0)):
                nc.gpsimd.tensor_scalar(
                    out=tab[:, q, :, wv, :], in0=sn[:, f], scalar1=sign, scalar2=0.0, op0=ALU.mult, op1=ALU.add
                )

        xc = []
        xs = []
        for pair in range(2):
            xc.append(const.tile([P, 2, 512], U32, name="xc%d" % pair, align_bytes=256))
            xs.append(const.tile([P, 2, 512], U8, name="xs%d" % pair, align_bytes=256))

        def turn(words, passes):
            bank = ps.tile([P, 2, 2, P], F32, name="tb", tag="ps")
            for i, g in enumerate(passes):
                for u in range(2):
                    nc.tensor.transpose(bank[:, u, i, :], words[:, 256 * g + u : 256 * (g + 1) : 2], ident[:])
            return bank

        HALVES = ((0, 1), (2, 3))

        def q_groups(s):
            mine = SCALAR_PASSES.get(s, ())
            groups = []
            for half in HALVES:
                for who in (False, True):
                    part = tuple(g for g in half if (g in mine) == who)
                    if part:
                        groups.append((who, part))
            return groups

        LAST0 = nc.vector if LAST_ON_V else nc.gpsimd
        banks = {}
        grxs = {}

        def x_quant(pair):
            nc.vector.quantize_mx(
                out=xc[pair][:].rearrange("p m k -> p (m k)").bitcast(FP8X4),
                scales=xs[pair][:].rearrange("p m k -> p (m k)"),
                in_=grxs[pair][:].rearrange("p m g r t -> p (m g r t)"),
            )

        w16 = {}
        gr = {}
        wc = {}
        ws = {}

        def cast(s, pieces=1):
            w16[s] = w16p.tile([P, K], BF16, name="w16", tag="w16", align_bytes=256)
            w = K // pieces
            for i in range(pieces):
                nc.scalar.copy(out=w16[s][:, w * i : w * (i + 1)], in_=wqb[s][:, w * i : w * (i + 1)].bitcast(FP8))

        def scale_on_vector(s, passes):
            g0, n = passes[0], len(passes)
            bank = banks["q", s, passes]
            nc.vector.tensor_tensor(
                out=gr[s][:, g0 : g0 + n, 0:P, :].rearrange("p g r (u e) -> p g r u e", e=2),
                in0=bank[:, :, 0:n, :].bitcast(BF16).rearrange("p u g (r e) -> p g r u e", e=2),
                in1=sc[:, g0 : g0 + n, :].rearrange("p g (u e) -> p g u e", e=2).unsqueeze(2).to_broadcast([P, n, P, 2, 2]),
                op=ALU.mult,
            )

        def scale_on_scalar(s, passes):
            planes = {}
            bv = banks["q", s, passes][:].bitcast(BF16).rearrange("p u g (r e) -> p g u e r", e=2)
            for i, g in enumerate(passes):
                planes[g] = plp.tile([P, 4, P], BF16, name="pl", tag="pl", align_bytes=256)
                for t in range(4):
                    nc.scalar.activation(
                        out=planes[g][:, t, :], in_=bv[:, i, t // 2, t % 2, :], func=ACTF.Copy, scale=sc[:, g, t : t + 1],
                    )
            return planes

        def interleave(s, g, planes):
            rows = IL_ROWS if g in G_IL else 0
            if rows:
                nc.gpsimd.tensor_scalar(
                    out=gr[s][:, g, 0:rows, :], in0=planes[:, :, 0:rows].rearrange("p t r -> p r t"),
                    scalar1=1.0, scalar2=0.0, op0=ALU.mult, op1=ALU.add,
                )
            if rows < P:
                nc.scalar.copy(
                    out=gr[s][:, g, rows:P, :].rearrange("p (c i) t -> p c t i", i=4),
                    in_=planes[:, :, rows:P].rearrange("p t (c i) -> p c t i", i=4),
                )

        def quant(s):
            wc[s] = wcp.tile([P, 4, 256], U32, name="wc", tag="wc", align_bytes=256)
            ws[s] = wcp.tile([P, 4, 256], U8, name="ws", tag="ws", align_bytes=256)
            nc.vector.quantize_mx(
                out=wc[s][:].rearrange("p g n -> p (g n)").bitcast(FP8X4),
                scales=ws[s][:].rearrange("p g n -> p (g n)"),
                in_=gr[s][:].rearrange("p g n t -> p (g n t)"),
            )

        def project(s, pair):
            acc = ps.tile([P, 2, 256], F32, name="acc", tag="ps")
            for mi in range(2):
                for g in range(4):
                    cols = slice(P * g, P * (g + 1))
                    nc.tensor.matmul_mx(
                        out=acc[:, mi, :],
                        lhsT=xc[pair][:, mi, cols].bitcast(FP8X4),
                        lhsT_scale=xs[pair][:, mi, cols],
                        rhs=wc[s][:, g, :].bitcast(FP8X4),
                        rhs_scale=ws[s][:, g, :],
                        start=(g == 0),
                        stop=(g == 3),
                    )
            return acc

        pqs = {}

        def rope(s, pair, acc):
            pq = rp.tile([P, 2, 4, 2, 64], F32, name="pq", tag="pq", align_bytes=256)
            nc.vector.tensor_tensor(
                out=pq[:].rearrange("p q (m h) w j -> p q m h (w j)", h=2),
                in0=acc[:].rearrange("p m (h d) -> p m h d", d=P).unsqueeze(1).to_broadcast([P, 2, 2, 2, P]),
                in1=tab[:].rearrange("p q a w j -> p q a (w j)").unsqueeze(3).to_broadcast([P, 2, 2, 2, P]),
                op=ALU.mult,
            )
            pqs[s, pair] = pq

        def finish(s, pair, adder):
            pq = pqs[s, pair]
            adder.tensor_tensor(out=pq[:, 0], in0=pq[:, 0], in1=pq[:, 1, :, ::-1, :], op=ALU.add)
            for o in range(2):
                nc.sync.dma_start(
                    out=outs[o][256 * pair : 256 * (pair + 1), P * s : P * (s + 1)].rearrange("(m p) d -> p m d", p=P),
                    in_=pq[:, 0].rearrange("p (m h) w j -> p m h (w j)", h=2)[:, :, o, :],
                )


        def turn_q(s):
            gr[s] = grp.tile([P, 4, 256, 4], BF16, name="gr", tag="gr", align_bytes=256)
            for who, part in q_groups(s):
                banks["q", s, part] = turn(w16[s][:].bitcast(F32), part)

        def turn_k(s):
            for gh in range(2):
                banks["k", s, gh] = turn(wkb[s][:].bitcast(F32), HALVES[gh])

        def turn_x(m):
            if m % 2 == 0:
                grxs[m // 2] = grxp.tile([P, 2, 4, P, 4], BF16, name="grx", tag="grx", align_bytes=256)
            for gh in range(2):
                banks["x", m, gh] = turn(xr[m][:].bitcast(F32), HALVES[gh])

        def copy_x(m, copier):
            for gh in range(2):
                copier(
                    out=grxs[m // 2][:].bitcast(F32)[:, m % 2, 2 * gh : 2 * gh + 2, :, :],
                    in_=banks["x", m, gh][:].rearrange("p u g r -> p g r u"),
                )

        def copy_k(s):
            for gh in range(2):
                nc.scalar.copy(
                    out=gr[s][:].bitcast(F32)[:, 2 * gh : 2 * gh + 2, P : 2 * P, :],
                    in_=banks["k", s, gh][:].rearrange("p u g r -> p g r u"),
                )

        on_vector = nc.vector.tensor_copy
        on_scalar = nc.scalar.copy
        XC = [on_vector if m in X_ON_VECTOR else on_scalar for m in range(4)]
        cast(0, 2)
        turn_q(0)
        scale_on_vector(0, (0, 1))
        table_step(0)
        scale_on_vector(0, (2, 3))
        table_step(1)
        turn_x(0)
        cast(1)
        copy_x(0, XC[0])
        turn_q(1)
        scale_on_vector(1, (0, 1))
        scale_on_vector(1, (2, 3))
        turn_x(1)
        copy_x(1, XC[1])
        x_quant(0)
        turn_k(0)
        tables_finish()
        copy_k(0)
        quant(0)
        cast(2)
        turn_k(1)
        copy_k(1)
        turn_x(2)
        copy_x(2, on_vector)
        quant(1)
        turn_x(3)
        copy_x(3, XC[3])
        cast(3)
        x_quant(1)
        for s in range(2, NSTEP + LAG):
            j = s - LAG
            accs = []
            if s + LOAD_AHEAD < NSTEP:
                load_q(s + LOAD_AHEAD)
                load_k(s + LOAD_AHEAD)
            if s < NSTEP:
                turn_q(s)
            accs.append(project(j, 0))
            if s < NSTEP:
                turn_k(s)
            accs.append(project(j, 1))
            if s < NSTEP:
                planes = {}
                for who, part in q_groups(s):
                    if who:
                        planes.update(scale_on_scalar(s, part))
                    else:
                        scale_on_vector(s, part)
                copy_k(s)
                for g in planes:
                    interleave(s, g, planes[g])
            if s + CAST_AHEAD < NSTEP:
                cast(s + CAST_AHEAD)
            rope(j, 0, accs[0])
            if j < NSTEP - 1:
                finish(j, 0, nc.gpsimd)
            if 2 < s < NSTEP:
                quant(s - 1)
            if s == NSTEP - 1:
                quant(s)
            rope(j, 1, accs[1])
            if j < NSTEP - 1:
                finish(j, 1, nc.gpsimd)
            else:
                finish(j, 0, nc.vector)
                finish(j, 1, nc.vector)
